import numpy as np
import ml_dtypes


def mxq(x, axis, fmt="e4m3"):
    dtype, down = {"e4m3": (ml_dtypes.float8_e4m3fn, 7), "e5m2": (ml_dtypes.float8_e5m2, 14)}[fmt]
    v = np.moveaxis(np.asarray(x, np.float32).astype(ml_dtypes.bfloat16).astype(np.float64), axis, -1)
    blocks = v.reshape(v.shape[:-1] + (-1, 32))
    amax = np.abs(blocks).max(-1, keepdims=True)
    byte = np.maximum(np.where(amax > 0, np.frexp(amax)[1] - 1 + 127, 0) - down, 1)
    scale = np.exp2(byte - 127.0)
    codes = (blocks / scale).astype(np.float32).astype(dtype).astype(np.float64)
    return np.moveaxis((codes * scale).reshape(v.shape), -1, axis)


WIDE = False


def mx_kscale(k):
    if not WIDE:
        return np.ones(k)
    levels = np.array([10, -10, 5, -5, 0])
    a = np.random.permutation(np.resize(levels, k // 512 * 4)).reshape(k // 512, 4)
    idx = np.arange(k)
    return np.exp2(a[idx // 512, idx % 128 // 32])


BF16 = ml_dtypes.bfloat16


def bf(x):
    return np.asarray(x, np.float32).astype(BF16)


def f64(x):
    return np.asarray(x).astype(np.float64)


B, N, D, C, H, NS = 4, 2048, 512, 256, 4, 11
HD = C // H
D4 = (0.4829629131445341, 0.8365163037378079, 0.2241438680420134, -0.1294095225512604)


def causal_multiscale(x_c, scale_gain):
    g = np.exp(scale_gain - scale_gain.max(0, keepdims=True))
    gains = g / g.sum(0, keepdims=True)
    gains_exp = np.repeat(gains, HD, axis=1)
    out = np.zeros_like(x_c)
    for j in range(NS):
        d = 2 ** j
        xp = np.pad(x_c, ((0, 0), (0, 0), (3 * d, 0)))
        y = (D4[0] * xp[:, :, 0 * d:0 * d + N]
             + D4[1] * xp[:, :, 1 * d:1 * d + N]
             + D4[2] * xp[:, :, 2 * d:2 * d + N]
             + D4[3] * xp[:, :, 3 * d:3 * d + N])
        out = out + gains_exp[j][None, :, None] * y
    return out


def setup_inputs():
    s = mx_kscale(D)
    return {"x": bf(np.random.standard_normal((B, N, D)) * s),
            "k_w": bf(np.random.standard_normal((C, D)) / np.sqrt(D) / s[None, :]),
            "k_b": bf(np.random.standard_normal(C) * 0.2),
            "v_w": bf(np.random.standard_normal((C, D)) / np.sqrt(D) / s[None, :]),
            "v_b": bf(np.random.standard_normal(C) * 0.2),
            "scale_gain": bf(np.random.standard_normal((NS, H)) * 0.5)}


def reference(x, k_w, k_b, v_w, v_b, scale_gain):
    xq = mxq(f64(x), 2, "e4m3")
    k = ((xq @ mxq(f64(k_w), 1, "e4m3").T) + f64(k_b)).reshape(B, N, H, HD)
    v = ((xq @ mxq(f64(v_w), 1, "e4m3").T) + f64(v_b)).reshape(B, N, H, HD)
    k_mag = np.sqrt((k * k).sum(-1, keepdims=True))
    field = v * k_mag
    x_c = field.transpose(0, 2, 3, 1).reshape(B, C, N)
    return causal_multiscale(x_c, f64(scale_gain))

@@ -1,0 +1,280 @@
+from contextlib import ExitStack
+
+import concourse.mybir as mybir
+from concourse.masks import make_identity
+
+F32 = mybir.dt.float32
+BF16 = mybir.dt.bfloat16
+U32 = mybir.dt.uint32
+U8 = mybir.dt.uint8
+FP8X4 = mybir.dt.float8_e4m3fn_x4
+ALU = mybir.AluOpType
+ACT = mybir.ActivationFunctionType
+AX = mybir.AxisListType
+
+P = 128
+B, N, D, C, H, NS = 4, 2048, 512, 256, 4, 11
+HD = C // H
+R = N // P
+TOK = 4 * P
+T0, T1, T2, T3 = 0.4829629131445341, 0.8365163037378079, 0.2241438680420134, -0.1294095225512604
+A0 = 32
+NHI = P - A0
+LATTICE_STEPS = (1, 2, 3, 4, 6, 8, 12, 16, 24, 32, 48, 64, 96)
+LOW_TAPS = (1, 2, 3, 4, 6, 8, 12, 24)
+
+FLOPS = 2 * B * N * D * 2 * C
+
+
+def tile_causalwaveletfieldattentionbyte_pa_t_kernel(tc, x, k_w, k_b, v_w, v_b, scale_gain, out):
+    nc = tc.nc
+    with ExitStack() as ctx:
+        const = ctx.enter_context(tc.tile_pool(name="const", bufs=1))
+        xpool = ctx.enter_context(tc.tile_pool(name="xpool", bufs=4))
+        stage = ctx.enter_context(tc.tile_pool(name="stage", bufs=2))
+        fpool = ctx.enter_context(tc.tile_pool(name="fpool", bufs=2))
+        opool = ctx.enter_context(tc.tile_pool(name="opool", bufs=3))
+        ps_tp = ctx.enter_context(tc.psum_pool(name="ps_tp", bufs=2))
+        ps_mm = ctx.enter_context(tc.psum_pool(name="ps_mm", bufs=3))
+        ps_hi = ctx.enter_context(tc.psum_pool(name="ps_hi", bufs=2))
+        ps_m2 = ctx.enter_context(tc.psum_pool(name="ps_m2", bufs=1))
+
+        w_sb = const.tile([P, 4 * D], BF16)
+        nc.sync.dma_start(
+            out=w_sb[:, 0 : 2 * D].rearrange("p (t k) -> p t k", t=2),
+            in_=k_w.rearrange("(t p) k -> p t k", p=P),
+        )
+        nc.sync.dma_start(
+            out=w_sb[:, 2 * D : 4 * D].rearrange("p (t k) -> p t k", t=2),
+            in_=v_w.rearrange("(t p) k -> p t k", p=P),
+        )
+        kb_rows = const.tile([2, P], BF16)
+        nc.scalar.dma_start(out=kb_rows[:], in_=k_b.rearrange("(g c) -> g c", g=2))
+        vb_bf = const.tile([P, C], BF16)
+        nc.scalar.dma_start(out=vb_bf[:], in_=v_b.partition_broadcast(P))
+        sg_bf = const.tile([P, NS * H], BF16)
+        nc.scalar.dma_start(out=sg_bf[:], in_=scale_gain.rearrange("j h -> (j h)").partition_broadcast(P))
+
+        x_words = []
+        for b in range(B):
+            x_sb = xpool.tile([P, R * D], BF16)
+            x_rows = x[b].rearrange("(a r) k -> a (r k)", r=R)
+            for q in range(4):
+                nc.sync.dma_start(
+                    out=x_sb[:, q * 4 * D : (q + 1) * 4 * D], in_=x_rows[:, q * 4 * D : (q + 1) * 4 * D]
+                )
+            x_words.append(x_sb[:].bitcast(F32).rearrange("p (r w) -> p r w", r=R))
+
+        ident = const.tile([P, P], F32)
+        make_identity(nc, ident[:])
+        shifts = const.tile([P, 2 * P], F32)
+        nc.vector.memset(shifts[:, 0:P], 0.0)
+        nc.vector.tensor_copy(out=shifts[:, P : 2 * P], in_=ident[:])
+
+        ind = const.tile([P, 2, H], F32)
+        nc.vector.memset(ind[:], 0.0)
+        for g in range(2):
+            nc.vector.memset(ind[0:64, g, 2 * g : 2 * g + 1], 1.0)
+            nc.vector.memset(ind[64:128, g, 2 * g + 1 : 2 * g + 2], 1.0)
+
+        w_words = w_sb[:].bitcast(F32).rearrange("p (t w) -> p t w", t=4)
+        w_grp = const.tile([P, 4 * 4 * P], BF16, align_bytes=64)
+        w_grp_words = w_grp[:].bitcast(F32).rearrange("p (c u) -> p c u", u=2)
+        for half in range(2):
+            wt = ps_tp.tile([P, 2, 2, P], F32, tag="tp")
+            for i in range(2):
+                for u in range(2):
+                    nc.tensor.transpose(wt[:, i, u, :], w_words[:, 2 * half + i, u * P : (u + 1) * P], ident[:])
+            nc.vector.tensor_copy(
+                out=w_grp_words[:, 2 * half * P : (2 * half + 2) * P, :].rearrange("p (i c) u -> p i c u", i=2),
+                in_=wt[:].rearrange("p i u c -> p i c u"),
+            )
+        w_codes = const.tile([P, 4 * P], U32, align_bytes=64)
+        w_scales = const.tile([P, 4 * P], U8, align_bytes=64)
+        nc.vector.quantize_mx(out=w_codes[:].bitcast(FP8X4), scales=w_scales[:], in_=w_grp[:])
+
+        kb_pad = const.tile([P, P], F32)
+        nc.vector.memset(kb_pad[:], 0.0)
+        nc.vector.tensor_copy(out=kb_pad[0:2, :], in_=kb_rows[:])
+        kb_ps = ps_tp.tile([P, P], F32, tag="tp")
+        nc.tensor.transpose(kb_ps[:], kb_pad[:], ident[:])
+        kb = const.tile([P, 2], F32)
+        nc.vector.tensor_copy(out=kb[:], in_=kb_ps[:, 0:2])
+        vb = const.tile([P, C], F32)
+        nc.vector.tensor_copy(out=vb[:], in_=vb_bf[:])
+
+        sg = const.tile([P, H, NS], F32)
+        nc.vector.tensor_copy(out=sg[:], in_=sg_bf[:].rearrange("p (j h) -> p h j", h=H))
+        top = const.tile([P, H], F32)
+        nc.vector.tensor_reduce(out=top[:], in_=sg[:], axis=AX.X, op=ALU.max)
+        nc.vector.tensor_tensor(
+            out=sg[:], in0=sg[:], in1=top[:].unsqueeze(2).to_broadcast([P, H, NS]), op=ALU.subtract
+        )
+        nc.scalar.activation(out=sg[:], in_=sg[:], func=ACT.Exp)
+        tot = const.tile([P, H], F32)
+        nc.vector.tensor_reduce(out=tot[:], in_=sg[:], axis=AX.X, op=ALU.add)
+        nc.vector.reciprocal(out=tot[:], in_=tot[:])
+        nc.vector.tensor_tensor(
+            out=sg[:], in0=sg[:], in1=tot[:].unsqueeze(2).to_broadcast([P, H, NS]), op=ALU.mult
+        )
+        pow2 = const.tile([P, H, NS], F32)
+        nc.vector.tensor_scalar_mul(out=pow2[:], in0=sg[:], scalar1=T2)
+        nc.vector.scalar_tensor_tensor(
+            out=pow2[:, :, 1:NS], in0=sg[:, :, 0 : NS - 1], scalar=T1, in1=pow2[:, :, 1:NS],
+            op0=ALU.mult, op1=ALU.add,
+        )
+        thr = const.tile([P, H, NS], F32)
+        nc.vector.tensor_scalar_mul(out=thr[:], in0=sg[:], scalar1=T0)
+
+        def coef(offset, h):
+            for j in range(NS):
+                if offset == 2**j:
+                    return pow2[:, h, j : j + 1]
+                if offset == 3 * 2**j:
+                    return thr[:, h, j : j + 1]
+            raise ValueError("no such tap")
+
+        toep = const.tile([P, H, NHI], F32)
+
+        def build_toeplitz():
+            for h in range(H):
+                nc.vector.tensor_scalar_mul(out=toep[:, h, :], in0=shifts[:, P + A0 : 2 * P], scalar1=T3)
+            for s in LATTICE_STEPS:
+                for h in range(H):
+                    nc.vector.scalar_tensor_tensor(
+                        out=toep[:, h, :], in0=shifts[:, P + A0 - s : 2 * P - s], scalar=coef(16 * s, h),
+                        in1=toep[:, h, :], op0=ALU.mult, op1=ALU.add,
+                    )
+
+        def group(b, q, field, early):
+            b2 = b % 2
+            x_grp = stage.tile([P, 4 * TOK], BF16, align_bytes=64)
+            x_grp_words = x_grp[:].bitcast(F32).rearrange("p (t u) -> p t u", u=2)
+            for half in range(2):
+                xt = ps_tp.tile([P, 2, 2, P], F32, tag="tp")
+                for i in range(2):
+                    for u in range(2):
+                        nc.tensor.transpose(
+                            xt[:, i, u, :], x_words[b][:, 4 * q + 2 * half + i, u * P : (u + 1) * P], ident[:]
+                        )
+                dst = x_grp_words[:, 2 * half * P : (2 * half + 2) * P, :].rearrange("p (i a) u -> p i a u", i=2)
+                src = xt[:].rearrange("p i u a -> p i a u")
+                if early:
+                    nc.vector.tensor_copy(out=dst, in_=src)
+                else:
+                    nc.scalar.copy(out=dst, in_=src)
+            x_codes = stage.tile([P, TOK], U32, align_bytes=64)
+            x_scales = stage.tile([P, TOK], U8, align_bytes=64)
+            nc.vector.quantize_mx(out=x_codes[:].bitcast(FP8X4), scales=x_scales[:], in_=x_grp[:])
+
+            k_sq = stage.tile([P, 2, TOK], F32)
+            for g in range(2):
+                k_ps = ps_mm.tile([P, TOK], F32, tag="mm")
+                nc.tensor.matmul_mx(
+                    out=k_ps[:],
+                    lhsT=w_codes[:, g * P : (g + 1) * P].bitcast(FP8X4),
+                    lhsT_scale=w_scales[:, g * P : (g + 1) * P],
+                    rhs=x_codes[:].bitcast(FP8X4),
+                    rhs_scale=x_scales[:],
+                    start=True,
+                    stop=True,
+                )
+                nc.scalar.activation(out=k_sq[:, g, :], in_=k_ps[:], func=ACT.Square, bias=kb[:, g : g + 1], scale=1.0)
+            m2 = ps_m2.tile([P, 4, H], F32, tag="m2")
+            for i in range(4):
+                for g in range(2):
+                    nc.tensor.matmul(
+                        out=m2[:, i, :], lhsT=k_sq[:, g, i * P : (i + 1) * P], rhs=ind[:, g, :],
+                        start=(g == 0), stop=(g == 1),
+                    )
+            mag = stage.tile([P, 4, H], F32)
+            nc.scalar.activation(out=mag[:], in_=m2[:], func=ACT.Sqrt)
+
+            for half in range(2):
+                v_ps = ps_mm.tile([P, 2, C], F32, tag="mm")
+                for i in range(2):
+                    t = 2 * half + i
+                    nc.tensor.matmul_mx(
+                        out=v_ps[:, i, :],
+                        lhsT=x_codes[:, t * P : (t + 1) * P].bitcast(FP8X4),
+                        lhsT_scale=x_scales[:, t * P : (t + 1) * P],
+                        rhs=w_codes[:, 2 * P : 4 * P].bitcast(FP8X4),
+                        rhs_scale=w_scales[:, 2 * P : 4 * P],
+                        start=True,
+                        stop=True,
+                    )
+                v_sum = stage.tile([P, 2, C], F32)
+                nc.vector.tensor_tensor(
+                    out=v_sum[:], in0=v_ps[:], in1=vb[:].unsqueeze(1).to_broadcast([P, 2, C]), op=ALU.add
+                )
+                r0 = 4 * q + 2 * half
+                if early:
+                    nc.vector.tensor_tensor(
+                        out=field[:, :, r0 : r0 + 2, b2 * HD : (b2 + 1) * HD].rearrange("p h i c -> p i h c"),
+                        in0=v_sum[:].rearrange("p i (h c) -> p i h c", h=H),
+                        in1=mag[:, 2 * half : 2 * half + 2, :].unsqueeze(3).to_broadcast([P, 2, H, HD]),
+                        op=ALU.mult,
+                    )
+                else:
+                    for i in range(2):
+                        for h in range(H):
+                            nc.scalar.activation(
+                                out=field[:, h, r0 + i, b2 * HD : (b2 + 1) * HD],
+                                in_=v_sum[:, i, h * HD : (h + 1) * HD],
+                                func=ACT.Copy,
+                                scale=mag[:, 2 * half + i, h : h + 1],
+                            )
+
+        def unit(pair, h, field):
+            f_t = opool.tile([P, N], F32, tag="f_t", bufs=2)
+            acc = opool.tile([P, N], F32, tag="acc")
+            f_view = f_t[:].rearrange("p (a r) -> p a r", r=R)
+            acc_view = acc[:].rearrange("p (a r) -> p a r", r=R)
+            for q in range(4):
+                tp = ps_tp.tile([P, 4, P], F32, tag="tp")
+                hi = ps_hi.tile([P, 4, NHI], F32, tag="hi")
+                for i in range(4):
+                    nc.tensor.transpose(tp[:, i, :], field[:, h, 4 * q + i, :], ident[:])
+                for i in range(4):
+                    nc.tensor.matmul(
+                        out=hi[:, i, :], lhsT=field[:, h, 4 * q + i, :], rhs=toep[:, h, :], start=True, stop=True
+                    )
+                tp_view = tp[:].rearrange("p i a -> p a i")
+                nc.scalar.copy(out=f_view[:, :, 4 * q : 4 * q + 4], in_=tp_view)
+                nc.scalar.activation(
+                    out=acc_view[:, 0:A0, 4 * q : 4 * q + 4], in_=tp_view[:, 0:A0, :], func=ACT.Copy, scale=T3
+                )
+                nc.scalar.copy(out=acc_view[:, A0:P, 4 * q : 4 * q + 4], in_=hi[:].rearrange("p i a -> p a i"))
+
+            first = [(o, o, N // 2) for o in LOW_TAPS]
+            first += [(16 * s, 16 * s, 16 * A0) for s in LATTICE_STEPS if s < A0]
+            second = [(o, N // 2, N) for o in LOW_TAPS]
+            ops = []
+            for i in range(len(first)):
+                ops.append(first[i])
+                if i < len(second):
+                    ops.append(second[i])
+            for o, lo, up in ops:
+                nc.vector.scalar_tensor_tensor(
+                    out=acc[:, lo:up], in0=f_t[:, lo - o : up - o], scalar=coef(o, h), in1=acc[:, lo:up],
+                    op0=ALU.mult, op1=ALU.add,
+                )
+            for b2 in range(2):
+                nc.sync.dma_start(
+                    out=out[2 * pair + b2, h * HD : (h + 1) * HD, :], in_=acc[b2 * HD : (b2 + 1) * HD, :]
+                )
+
+        field0 = fpool.tile([P, H, R, P], F32, tag="field")
+        for q in range(4):
+            group(0, q, field0, True)
+        build_toeplitz()
+        for q in range(4):
+            group(1, q, field0, True)
+        field1 = fpool.tile([P, H, R, P], F32, tag="field")
+        for h in range(H):
+            unit(0, h, field0)
+            for j in range(2):
+                step = 2 * h + j
+                group(2 + step // 4, step % 4, field1, False)
+        for h in range(H):
+            unit(1, h, field1)

@@ -17,11 +17,15 @@ B, N, D, C, H, NS = 4, 2048, 512, 256, 4, 11
 HD = C // H
 R = N // P
 TOK = 4 * P
+BANK = 512
 T0, T1, T2, T3 = 0.4829629131445341, 0.8365163037378079, 0.2241438680420134, -0.1294095225512604
 A0 = 32
 NHI = P - A0
+HEAD = 16 * A0
 LATTICE_STEPS = (1, 2, 3, 4, 6, 8, 12, 16, 24, 32, 48, 64, 96)
-LOW_TAPS = (1, 2, 3, 4, 6, 8, 12, 24)
+V_TAPS = (1, 2, 3, 6, 8)
+LAST_TAP = 4
+G_TAPS = (12, 24)
 
 FLOPS = 2 * B * N * D * 2 * C
 
@@ -30,101 +34,21 @@ def tile_causalwaveletfieldattentionbyte_pa_t_kernel(tc, x, k_w, k_b, v_w, v_b, 
     nc = tc.nc
     with ExitStack() as ctx:
         const = ctx.enter_context(tc.tile_pool(name="const", bufs=1))
-        xpool = ctx.enter_context(tc.tile_pool(name="xpool", bufs=4))
-        stage = ctx.enter_context(tc.tile_pool(name="stage", bufs=2))
-        fpool = ctx.enter_context(tc.tile_pool(name="fpool", bufs=2))
-        opool = ctx.enter_context(tc.tile_pool(name="opool", bufs=3))
-        ps_tp = ctx.enter_context(tc.psum_pool(name="ps_tp", bufs=2))
-        ps_mm = ctx.enter_context(tc.psum_pool(name="ps_mm", bufs=3))
-        ps_hi = ctx.enter_context(tc.psum_pool(name="ps_hi", bufs=2))
-        ps_m2 = ctx.enter_context(tc.psum_pool(name="ps_m2", bufs=1))
+        psum = ctx.enter_context(tc.psum_pool(name="psum", bufs=1))
+        turn = [0]
 
-        w_sb = const.tile([P, 4 * D], BF16)
-        nc.sync.dma_start(
-            out=w_sb[:, 0 : 2 * D].rearrange("p (t k) -> p t k", t=2),
-            in_=k_w.rearrange("(t p) k -> p t k", p=P),
-        )
-        nc.sync.dma_start(
-            out=w_sb[:, 2 * D : 4 * D].rearrange("p (t k) -> p t k", t=2),
-            in_=v_w.rearrange("(t p) k -> p t k", p=P),
-        )
-        kb_rows = const.tile([2, P], BF16)
-        nc.scalar.dma_start(out=kb_rows[:], in_=k_b.rearrange("(g c) -> g c", g=2))
-        vb_bf = const.tile([P, C], BF16)
-        nc.scalar.dma_start(out=vb_bf[:], in_=v_b.partition_broadcast(P))
-        sg_bf = const.tile([P, NS * H], BF16)
-        nc.scalar.dma_start(out=sg_bf[:], in_=scale_gain.rearrange("j h -> (j h)").partition_broadcast(P))
+        def bank(k):
+            return psum.tile([P, BANK], F32, name="bank%d" % k, tag="bank%d" % k)
 
-        x_words = []
-        for b in range(B):
-            x_sb = xpool.tile([P, R * D], BF16)
-            x_rows = x[b].rearrange("(a r) k -> a (r k)", r=R)
-            for q in range(4):
-                nc.sync.dma_start(
-                    out=x_sb[:, q * 4 * D : (q + 1) * 4 * D], in_=x_rows[:, q * 4 * D : (q + 1) * 4 * D]
-                )
-            x_words.append(x_sb[:].bitcast(F32).rearrange("p (r w) -> p r w", r=R))
+        def next_bank(first, count):
+            turn[0] += 1
+            return bank(first + turn[0] % count)
 
+        fields = [const.tile([P, H, R, P], F32, name="field%d" % pair) for pair in range(2)]
         ident = const.tile([P, P], F32)
-        make_identity(nc, ident[:])
-        shifts = const.tile([P, 2 * P], F32)
-        nc.vector.memset(shifts[:, 0:P], 0.0)
-        nc.vector.tensor_copy(out=shifts[:, P : 2 * P], in_=ident[:])
-
-        ind = const.tile([P, 2, H], F32)
-        nc.vector.memset(ind[:], 0.0)
-        for g in range(2):
-            nc.vector.memset(ind[0:64, g, 2 * g : 2 * g + 1], 1.0)
-            nc.vector.memset(ind[64:128, g, 2 * g + 1 : 2 * g + 2], 1.0)
-
-        w_words = w_sb[:].bitcast(F32).rearrange("p (t w) -> p t w", t=4)
-        w_grp = const.tile([P, 4 * 4 * P], BF16, align_bytes=64)
-        w_grp_words = w_grp[:].bitcast(F32).rearrange("p (c u) -> p c u", u=2)
-        for half in range(2):
-            wt = ps_tp.tile([P, 2, 2, P], F32, tag="tp")
-            for i in range(2):
-                for u in range(2):
-                    nc.tensor.transpose(wt[:, i, u, :], w_words[:, 2 * half + i, u * P : (u + 1) * P], ident[:])
-            nc.vector.tensor_copy(
-                out=w_grp_words[:, 2 * half * P : (2 * half + 2) * P, :].rearrange("p (i c) u -> p i c u", i=2),
-                in_=wt[:].rearrange("p i u c -> p i c u"),
-            )
-        w_codes = const.tile([P, 4 * P], U32, align_bytes=64)
-        w_scales = const.tile([P, 4 * P], U8, align_bytes=64)
-        nc.vector.quantize_mx(out=w_codes[:].bitcast(FP8X4), scales=w_scales[:], in_=w_grp[:])
-
-        kb_pad = const.tile([P, P], F32)
-        nc.vector.memset(kb_pad[:], 0.0)
-        nc.vector.tensor_copy(out=kb_pad[0:2, :], in_=kb_rows[:])
-        kb_ps = ps_tp.tile([P, P], F32, tag="tp")
-        nc.tensor.transpose(kb_ps[:], kb_pad[:], ident[:])
-        kb = const.tile([P, 2], F32)
-        nc.vector.tensor_copy(out=kb[:], in_=kb_ps[:, 0:2])
-        vb = const.tile([P, C], F32)
-        nc.vector.tensor_copy(out=vb[:], in_=vb_bf[:])
-
-        sg = const.tile([P, H, NS], F32)
-        nc.vector.tensor_copy(out=sg[:], in_=sg_bf[:].rearrange("p (j h) -> p h j", h=H))
-        top = const.tile([P, H], F32)
-        nc.vector.tensor_reduce(out=top[:], in_=sg[:], axis=AX.X, op=ALU.max)
-        nc.vector.tensor_tensor(
-            out=sg[:], in0=sg[:], in1=top[:].unsqueeze(2).to_broadcast([P, H, NS]), op=ALU.subtract
-        )
-        nc.scalar.activation(out=sg[:], in_=sg[:], func=ACT.Exp)
-        tot = const.tile([P, H], F32)
-        nc.vector.tensor_reduce(out=tot[:], in_=sg[:], axis=AX.X, op=ALU.add)
-        nc.vector.reciprocal(out=tot[:], in_=tot[:])
-        nc.vector.tensor_tensor(
-            out=sg[:], in0=sg[:], in1=tot[:].unsqueeze(2).to_broadcast([P, H, NS]), op=ALU.mult
-        )
         pow2 = const.tile([P, H, NS], F32)
-        nc.vector.tensor_scalar_mul(out=pow2[:], in0=sg[:], scalar1=T2)
-        nc.vector.scalar_tensor_tensor(
-            out=pow2[:, :, 1:NS], in0=sg[:, :, 0 : NS - 1], scalar=T1, in1=pow2[:, :, 1:NS],
-            op0=ALU.mult, op1=ALU.add,
-        )
         thr = const.tile([P, H, NS], F32)
-        nc.vector.tensor_scalar_mul(out=thr[:], in0=sg[:], scalar1=T0)
+        toep = const.tile([P, H, NHI], F32)
 
         def coef(offset, h):
             for j in range(NS):
@@ -134,147 +58,264 @@ def tile_causalwaveletfieldattentionbyte_pa_t_kernel(tc, x, k_w, k_b, v_w, v_b, 
                     return thr[:, h, j : j + 1]
             raise ValueError("no such tap")
 
-        toep = const.tile([P, H, NHI], F32)
-
-        def build_toeplitz():
-            for h in range(H):
-                nc.vector.tensor_scalar_mul(out=toep[:, h, :], in0=shifts[:, P + A0 : 2 * P], scalar1=T3)
-            for s in LATTICE_STEPS:
-                for h in range(H):
-                    nc.vector.scalar_tensor_tensor(
-                        out=toep[:, h, :], in0=shifts[:, P + A0 - s : 2 * P - s], scalar=coef(16 * s, h),
-                        in1=toep[:, h, :], op0=ALU.mult, op1=ALU.add,
+        with tc.tile_pool(name="once", bufs=1) as once, tc.tile_pool(name="stage", bufs=3) as stage:
+            w_sb = once.tile([P, 4 * D], BF16)
+            nc.sync.dma_start(
+                out=w_sb[:, 0 : 2 * D].rearrange("p (t k) -> p t k", t=2),
+                in_=k_w.rearrange("(t p) k -> p t k", p=P),
+            )
+            nc.sync.dma_start(
+                out=w_sb[:, 2 * D : 4 * D].rearrange("p (t k) -> p t k", t=2),
+                in_=v_w.rearrange("(t p) k -> p t k", p=P),
+            )
+            kb_rows = once.tile([2, P], BF16)
+            nc.scalar.dma_start(out=kb_rows[:], in_=k_b.rearrange("(g c) -> g c", g=2))
+            vb_bf = once.tile([P, C], BF16)
+            nc.scalar.dma_start(out=vb_bf[:], in_=v_b.partition_broadcast(P))
+            sg_bf = once.tile([P, NS * H], BF16)
+            nc.scalar.dma_start(out=sg_bf[:], in_=scale_gain.rearrange("j h -> (j h)").partition_broadcast(P))
+            x_words = []
+            for b in range(B):
+                x_sb = once.tile([P, R * D], BF16, name="x_sb%d" % b)
+                x_rows = x[b].rearrange("(a r) k -> a (r k)", r=R)
+                for q in range(4):
+                    nc.sync.dma_start(
+                        out=x_sb[:, q * 4 * D : (q + 1) * 4 * D], in_=x_rows[:, q * 4 * D : (q + 1) * 4 * D]
                     )
+                x_words.append(x_sb[:].bitcast(F32).rearrange("p (r w) -> p r w", r=R))
 
-        def group(b, q, field, early):
-            b2 = b % 2
-            x_grp = stage.tile([P, 4 * TOK], BF16, align_bytes=64)
-            x_grp_words = x_grp[:].bitcast(F32).rearrange("p (t u) -> p t u", u=2)
+            make_identity(nc, ident[:])
+            shifts = once.tile([P, 2 * P], F32)
+            nc.vector.memset(shifts[:, 0:P], 0.0)
+            nc.vector.tensor_copy(out=shifts[:, P : 2 * P], in_=ident[:])
+            ind = once.tile([P, 2, H], F32)
+            nc.vector.memset(ind[:], 0.0)
+            for g in range(2):
+                nc.vector.memset(ind[0:64, g, 2 * g : 2 * g + 1], 1.0)
+                nc.vector.memset(ind[64:128, g, 2 * g + 1 : 2 * g + 2], 1.0)
+
+            w_words = w_sb[:].bitcast(F32).rearrange("p (t w) -> p t w", t=4)
+            w_grp = once.tile([P, 4 * 4 * P], BF16, align_bytes=64)
+            w_grp_words = w_grp[:].bitcast(F32).rearrange("p (c u) -> p c u", u=2)
             for half in range(2):
-                xt = ps_tp.tile([P, 2, 2, P], F32, tag="tp")
+                wt = bank(half)[:].rearrange("p (i u c) -> p i u c", i=2, u=2)
                 for i in range(2):
                     for u in range(2):
-                        nc.tensor.transpose(
-                            xt[:, i, u, :], x_words[b][:, 4 * q + 2 * half + i, u * P : (u + 1) * P], ident[:]
-                        )
-                dst = x_grp_words[:, 2 * half * P : (2 * half + 2) * P, :].rearrange("p (i a) u -> p i a u", i=2)
-                src = xt[:].rearrange("p i u a -> p i a u")
-                if early:
-                    nc.vector.tensor_copy(out=dst, in_=src)
-                else:
-                    nc.scalar.copy(out=dst, in_=src)
-            x_codes = stage.tile([P, TOK], U32, align_bytes=64)
-            x_scales = stage.tile([P, TOK], U8, align_bytes=64)
-            nc.vector.quantize_mx(out=x_codes[:].bitcast(FP8X4), scales=x_scales[:], in_=x_grp[:])
-
-            k_sq = stage.tile([P, 2, TOK], F32)
-            for g in range(2):
-                k_ps = ps_mm.tile([P, TOK], F32, tag="mm")
-                nc.tensor.matmul_mx(
-                    out=k_ps[:],
-                    lhsT=w_codes[:, g * P : (g + 1) * P].bitcast(FP8X4),
-                    lhsT_scale=w_scales[:, g * P : (g + 1) * P],
-                    rhs=x_codes[:].bitcast(FP8X4),
-                    rhs_scale=x_scales[:],
-                    start=True,
-                    stop=True,
+                        nc.tensor.transpose(wt[:, i, u, :], w_words[:, 2 * half + i, u * P : (u + 1) * P], ident[:])
+                nc.vector.tensor_copy(
+                    out=w_grp_words[:, 2 * half * P : (2 * half + 2) * P, :].rearrange("p (i c) u -> p i c u", i=2),
+                    in_=wt.rearrange("p i u c -> p i c u"),
                 )
-                nc.scalar.activation(out=k_sq[:, g, :], in_=k_ps[:], func=ACT.Square, bias=kb[:, g : g + 1], scale=1.0)
-            m2 = ps_m2.tile([P, 4, H], F32, tag="m2")
-            for i in range(4):
-                for g in range(2):
-                    nc.tensor.matmul(
-                        out=m2[:, i, :], lhsT=k_sq[:, g, i * P : (i + 1) * P], rhs=ind[:, g, :],
-                        start=(g == 0), stop=(g == 1),
-                    )
-            mag = stage.tile([P, 4, H], F32)
-            nc.scalar.activation(out=mag[:], in_=m2[:], func=ACT.Sqrt)
+            w_codes = once.tile([P, 4 * P], U32, align_bytes=64)
+            w_scales = once.tile([P, 4 * P], U8, align_bytes=64)
+            nc.vector.quantize_mx(out=w_codes[:].bitcast(FP8X4), scales=w_scales[:], in_=w_grp[:])
 
-            for half in range(2):
-                v_ps = ps_mm.tile([P, 2, C], F32, tag="mm")
-                for i in range(2):
-                    t = 2 * half + i
+            kb_pad = once.tile([P, P], F32)
+            nc.vector.memset(kb_pad[:], 0.0)
+            nc.vector.tensor_copy(out=kb_pad[0:2, :], in_=kb_rows[:])
+            kb_ps = bank(2)
+            nc.tensor.transpose(kb_ps[:, 0:P], kb_pad[:], ident[:])
+            kb = once.tile([P, 2], F32)
+            nc.vector.tensor_copy(out=kb[:], in_=kb_ps[:, 0:2])
+            vb = once.tile([P, C], F32)
+            nc.vector.tensor_copy(out=vb[:], in_=vb_bf[:])
+
+            sg = once.tile([P, H, NS], F32)
+            nc.vector.tensor_copy(out=sg[:], in_=sg_bf[:].rearrange("p (j h) -> p h j", h=H))
+            top = once.tile([P, H], F32)
+            nc.vector.tensor_reduce(out=top[:], in_=sg[:], axis=AX.X, op=ALU.max)
+            nc.vector.tensor_tensor(
+                out=sg[:], in0=sg[:], in1=top[:].unsqueeze(2).to_broadcast([P, H, NS]), op=ALU.subtract
+            )
+            nc.scalar.activation(out=sg[:], in_=sg[:], func=ACT.Exp)
+            tot = once.tile([P, H], F32)
+            nc.vector.tensor_reduce(out=tot[:], in_=sg[:], axis=AX.X, op=ALU.add)
+            nc.vector.reciprocal(out=tot[:], in_=tot[:])
+            nc.vector.tensor_tensor(
+                out=sg[:], in0=sg[:], in1=tot[:].unsqueeze(2).to_broadcast([P, H, NS]), op=ALU.mult
+            )
+            nc.vector.tensor_scalar_mul(out=pow2[:], in0=sg[:], scalar1=T2)
+            nc.vector.scalar_tensor_tensor(
+                out=pow2[:, :, 1:NS], in0=sg[:, :, 0 : NS - 1], scalar=T1, in1=pow2[:, :, 1:NS],
+                op0=ALU.mult, op1=ALU.add,
+            )
+            nc.vector.tensor_scalar_mul(out=thr[:], in0=sg[:], scalar1=T0)
+
+            def group(b, q):
+                field = fields[b // 2]
+                b2 = b % 2
+                x_grp = stage.tile([P, 4 * TOK], BF16, align_bytes=64)
+                x_grp_words = x_grp[:].bitcast(F32).rearrange("p (t u) -> p t u", u=2)
+                for half in range(2):
+                    xt = bank((2 * q + half) % 4)[:].rearrange("p (i u a) -> p i u a", i=2, u=2)
+                    for i in range(2):
+                        for u in range(2):
+                            nc.tensor.transpose(
+                                xt[:, i, u, :], x_words[b][:, 4 * q + 2 * half + i, u * P : (u + 1) * P], ident[:]
+                            )
+                    nc.scalar.copy(
+                        out=x_grp_words[:, 2 * half * P : (2 * half + 2) * P, :].rearrange(
+                            "p (i a) u -> p i a u", i=2
+                        ),
+                        in_=xt.rearrange("p i u a -> p i a u"),
+                    )
+                x_codes = stage.tile([P, TOK], U32, align_bytes=64)
+                x_scales = stage.tile([P, TOK], U8, align_bytes=64)
+                nc.vector.quantize_mx(out=x_codes[:].bitcast(FP8X4), scales=x_scales[:], in_=x_grp[:])
+
+                k_sq = stage.tile([P, 2, TOK], F32)
+                for g in range(2):
+                    k_ps = next_bank(4, 3)
                     nc.tensor.matmul_mx(
-                        out=v_ps[:, i, :],
-                        lhsT=x_codes[:, t * P : (t + 1) * P].bitcast(FP8X4),
-                        lhsT_scale=x_scales[:, t * P : (t + 1) * P],
-                        rhs=w_codes[:, 2 * P : 4 * P].bitcast(FP8X4),
-                        rhs_scale=w_scales[:, 2 * P : 4 * P],
+                        out=k_ps[:],
+                        lhsT=w_codes[:, g * P : (g + 1) * P].bitcast(FP8X4),
+                        lhsT_scale=w_scales[:, g * P : (g + 1) * P],
+                        rhs=x_codes[:].bitcast(FP8X4),
+                        rhs_scale=x_scales[:],
                         start=True,
                         stop=True,
                     )
-                v_sum = stage.tile([P, 2, C], F32)
-                nc.vector.tensor_tensor(
-                    out=v_sum[:], in0=v_ps[:], in1=vb[:].unsqueeze(1).to_broadcast([P, 2, C]), op=ALU.add
-                )
-                r0 = 4 * q + 2 * half
-                if early:
+                    nc.scalar.activation(
+                        out=k_sq[:, g, :], in_=k_ps[:], func=ACT.Square, bias=kb[:, g : g + 1], scale=1.0
+                    )
+                m2 = bank(7)[:, 0 : 4 * H].rearrange("p (i h) -> p i h", i=4)
+                for i in range(4):
+                    for g in range(2):
+                        nc.tensor.matmul(
+                            out=m2[:, i, :], lhsT=k_sq[:, g, i * P : (i + 1) * P], rhs=ind[:, g, :],
+                            start=(g == 0), stop=(g == 1),
+                        )
+                mag = stage.tile([P, 4, H], F32)
+                nc.scalar.activation(out=mag[:], in_=m2, func=ACT.Sqrt)
+
+                for half in range(2):
+                    v_ps = next_bank(4, 3)[:].rearrange("p (i c) -> p i c", i=2)
+                    for i in range(2):
+                        t = 2 * half + i
+                        nc.tensor.matmul_mx(
+                            out=v_ps[:, i, :],
+                            lhsT=x_codes[:, t * P : (t + 1) * P].bitcast(FP8X4),
+                            lhsT_scale=x_scales[:, t * P : (t + 1) * P],
+                            rhs=w_codes[:, 2 * P : 4 * P].bitcast(FP8X4),
+                            rhs_scale=w_scales[:, 2 * P : 4 * P],
+                            start=True,
+                            stop=True,
+                        )
+                    v_sum = stage.tile([P, 2, C], F32)
                     nc.vector.tensor_tensor(
+                        out=v_sum[:], in0=v_ps, in1=vb[:].unsqueeze(1).to_broadcast([P, 2, C]), op=ALU.add
+                    )
+                    r0 = 4 * q + 2 * half
+                    nc.gpsimd.tensor_tensor(
                         out=field[:, :, r0 : r0 + 2, b2 * HD : (b2 + 1) * HD].rearrange("p h i c -> p i h c"),
                         in0=v_sum[:].rearrange("p i (h c) -> p i h c", h=H),
                         in1=mag[:, 2 * half : 2 * half + 2, :].unsqueeze(3).to_broadcast([P, 2, H, HD]),
                         op=ALU.mult,
                     )
-                else:
-                    for i in range(2):
+
+            for b in range(B):
+                for q in range(4):
+                    group(b, q)
+                if b == 0:
+                    for h in range(H):
+                        nc.vector.tensor_scalar_mul(out=toep[:, h, :], in0=shifts[:, P + A0 : 2 * P], scalar1=T3)
+                    for s in LATTICE_STEPS:
                         for h in range(H):
-                            nc.scalar.activation(
-                                out=field[:, h, r0 + i, b2 * HD : (b2 + 1) * HD],
-                                in_=v_sum[:, i, h * HD : (h + 1) * HD],
-                                func=ACT.Copy,
-                                scale=mag[:, 2 * half + i, h : h + 1],
+                            nc.vector.scalar_tensor_tensor(
+                                out=toep[:, h, :], in0=shifts[:, P + A0 - s : 2 * P - s], scalar=coef(16 * s, h),
+                                in1=toep[:, h, :], op0=ALU.mult, op1=ALU.add,
                             )
 
-        def unit(pair, h, field):
-            f_t = opool.tile([P, N], F32, tag="f_t", bufs=2)
-            acc = opool.tile([P, N], F32, tag="acc")
-            f_view = f_t[:].rearrange("p (a r) -> p a r", r=R)
-            acc_view = acc[:].rearrange("p (a r) -> p a r", r=R)
-            for q in range(4):
-                tp = ps_tp.tile([P, 4, P], F32, tag="tp")
-                hi = ps_hi.tile([P, 4, NHI], F32, tag="hi")
-                for i in range(4):
-                    nc.tensor.transpose(tp[:, i, :], field[:, h, 4 * q + i, :], ident[:])
-                for i in range(4):
-                    nc.tensor.matmul(
-                        out=hi[:, i, :], lhsT=field[:, h, 4 * q + i, :], rhs=toep[:, h, :], start=True, stop=True
+        def runs(q, o):
+            res = []
+            for i in range(4):
+                carry, r = divmod(4 * q + i + o, R)
+                if res and res[-1][3] == carry:
+                    res[-1] = (res[-1][0], res[-1][1] + 1, res[-1][2], carry)
+                else:
+                    res.append((i, 1, r, carry))
+            return res
+
+        head_steps = [s for s in LATTICE_STEPS if s < A0]
+
+        with tc.tile_pool(name="opool", bufs=2) as opool:
+
+            def unit(pair, h):
+                field = fields[pair]
+                accp = opool.tile([P, R, P], F32, tag="accp", bufs=3)
+                nat = opool.tile([P, N], F32, tag="nat", bufs=3)
+                nat_view = nat[:].rearrange("p (a r) -> p a r", r=R)
+                f_head = opool.tile([P, HEAD], F32, tag="f_head")
+                f_head_view = f_head[:].rearrange("p (a r) -> p a r", r=R)
+                s_head = opool.tile([P, len(head_steps), HEAD], F32, tag="s_head")
+                scaled = {}
+                for o in G_TAPS:
+                    scaled[o] = opool.tile([P, N], F32, name="scaled%d" % o, tag="scaled%d" % o)
+                for q in range(4):
+                    hi = next_bank(4, 4)[:, 0 : 4 * NHI].rearrange("p (i a) -> p i a", i=4)
+                    for i in range(4):
+                        nc.tensor.matmul(
+                            out=hi[:, i, :], lhsT=field[:, h, 4 * q + i, :], rhs=toep[:, h, :], start=True, stop=True
+                        )
+                    nc.scalar.copy(out=accp[:, 4 * q : 4 * q + 4, A0:P], in_=hi)
+                tps = []
+                for q in range(4):
+                    tp = bank(q)[:].rearrange("p (i a) -> p i a", i=4)
+                    tps.append(tp)
+                    for i in range(4):
+                        nc.tensor.transpose(tp[:, i, :], field[:, h, 4 * q + i, :], ident[:])
+                    nc.scalar.activation(
+                        out=accp[:, 4 * q : 4 * q + 4, 0:A0], in_=tp[:, :, 0:A0], func=ACT.Copy, scale=T3
                     )
-                tp_view = tp[:].rearrange("p i a -> p a i")
-                nc.scalar.copy(out=f_view[:, :, 4 * q : 4 * q + 4], in_=tp_view)
-                nc.scalar.activation(
-                    out=acc_view[:, 0:A0, 4 * q : 4 * q + 4], in_=tp_view[:, 0:A0, :], func=ACT.Copy, scale=T3
-                )
-                nc.scalar.copy(out=acc_view[:, A0:P, 4 * q : 4 * q + 4], in_=hi[:].rearrange("p i a -> p a i"))
+                for q in range(4):
+                    tp_view = tps[q].rearrange("p i a -> p a i")
+                    nc.scalar.copy(out=f_head_view[:, :, 4 * q : 4 * q + 4], in_=tp_view[:, 0:A0, :])
+                    for o in G_TAPS:
+                        nc.scalar.activation(
+                            out=scaled[o][:].rearrange("p (a r) -> p a r", r=R)[:, :, 4 * q : 4 * q + 4],
+                            in_=tp_view, func=ACT.Copy, scale=coef(o, h),
+                        )
+                for k, s in enumerate(head_steps):
+                    width = HEAD - 16 * s
+                    nc.scalar.activation(
+                        out=s_head[:, k, 0:width], in_=f_head[:, 0:width], func=ACT.Copy, scale=coef(16 * s, h)
+                    )
+                for o in V_TAPS:
+                    for q in range(4):
+                        for i0, cnt, r0, carry in runs(q, o):
+                            nc.vector.scalar_tensor_tensor(
+                                out=accp[:, r0 : r0 + cnt, carry:P],
+                                in0=tps[q][:, i0 : i0 + cnt, 0 : P - carry],
+                                scalar=coef(o, h),
+                                in1=accp[:, r0 : r0 + cnt, carry:P],
+                                op0=ALU.mult, op1=ALU.add,
+                            )
+                for q in range(4):
+                    for i0, cnt, r0, carry in runs(q, LAST_TAP):
+                        nc.vector.scalar_tensor_tensor(
+                            out=nat_view[:, carry:P, r0 : r0 + cnt],
+                            in0=tps[q][:, i0 : i0 + cnt, 0 : P - carry].rearrange("p i a -> p a i"),
+                            scalar=coef(LAST_TAP, h),
+                            in1=accp[:, r0 : r0 + cnt, carry:P].rearrange("p r a -> p a r"),
+                            op0=ALU.mult, op1=ALU.add,
+                        )
+                        if carry:
+                            nc.vector.tensor_copy(
+                                out=nat_view[:, 0:carry, r0 : r0 + cnt],
+                                in_=accp[:, r0 : r0 + cnt, 0:carry].rearrange("p r a -> p a r"),
+                            )
+                for o in G_TAPS:
+                    nc.gpsimd.tensor_tensor(out=nat[:, o:N], in0=nat[:, o:N], in1=scaled[o][:, 0 : N - o], op=ALU.add)
+                for k, s in enumerate(head_steps):
+                    nc.gpsimd.tensor_tensor(
+                        out=nat[:, 16 * s : HEAD], in0=nat[:, 16 * s : HEAD], in1=s_head[:, k, 0 : HEAD - 16 * s],
+                        op=ALU.add,
+                    )
+                for b2 in range(2):
+                    nc.sync.dma_start(
+                        out=out[2 * pair + b2, h * HD : (h + 1) * HD, :], in_=nat[b2 * HD : (b2 + 1) * HD, :]
+                    )
 
-            first = [(o, o, N // 2) for o in LOW_TAPS]
-            first += [(16 * s, 16 * s, 16 * A0) for s in LATTICE_STEPS if s < A0]
-            second = [(o, N // 2, N) for o in LOW_TAPS]
-            ops = []
-            for i in range(len(first)):
-                ops.append(first[i])
-                if i < len(second):
-                    ops.append(second[i])
-            for o, lo, up in ops:
-                nc.vector.scalar_tensor_tensor(
-                    out=acc[:, lo:up], in0=f_t[:, lo - o : up - o], scalar=coef(o, h), in1=acc[:, lo:up],
-                    op0=ALU.mult, op1=ALU.add,
-                )
-            for b2 in range(2):
-                nc.sync.dma_start(
-                    out=out[2 * pair + b2, h * HD : (h + 1) * HD, :], in_=acc[b2 * HD : (b2 + 1) * HD, :]
-                )
-
-        field0 = fpool.tile([P, H, R, P], F32, tag="field")
-        for q in range(4):
-            group(0, q, field0, True)
-        build_toeplitz()
-        for q in range(4):
-            group(1, q, field0, True)
-        field1 = fpool.tile([P, H, R, P], F32, tag="field")
-        for h in range(H):
-            unit(0, h, field0)
-            for j in range(2):
-                step = 2 * h + j
-                group(2 + step // 4, step % 4, field1, False)
-        for h in range(H):
-            unit(1, h, field1)
+            for pair in range(2):
+                for h in range(H):
+                    unit(pair, h)

@@ -23,9 +23,10 @@ A0 = 32
 NHI = P - A0
 HEAD = 16 * A0
 LATTICE_STEPS = (1, 2, 3, 4, 6, 8, 12, 16, 24, 32, 48, 64, 96)
+PE_TAPS = (12, 24)
 V_TAPS = (1, 2, 3, 6, 8)
 LAST_TAP = 4
-G_TAPS = (12, 24)
+UNITS = 2 * H
 
 FLOPS = 2 * B * N * D * 2 * C
 
@@ -46,6 +47,8 @@ def tile_causalwaveletfieldattentionbyte_pa_t_kernel(tc, x, k_w, k_b, v_w, v_b, 
 
         fields = [const.tile([P, H, R, P], F32, name="field%d" % pair) for pair in range(2)]
         ident = const.tile([P, P], F32)
+        shifts = const.tile([P, 2 * P], F32)
+        wrap = const.tile([P, 2 * P], F32)
         pow2 = const.tile([P, H, NS], F32)
         thr = const.tile([P, H, NS], F32)
         toep = const.tile([P, H, NHI], F32)
@@ -58,25 +61,59 @@ def tile_causalwaveletfieldattentionbyte_pa_t_kernel(tc, x, k_w, k_b, v_w, v_b, 
                     return thr[:, h, j : j + 1]
             raise ValueError("no such tap")
 
+        ahead = ctx.enter_context(tc.tile_pool(name="ahead", bufs=3))
+        accps, f_scaleds = {}, {}
+
+        def scale_field(u):
+            pair, h = divmod(u, H)
+            for o in PE_TAPS:
+                f_scaleds[u, o] = ahead.tile([P, R, P], F32, name="f_scaled%d" % o, tag="f_scaled%d" % o)
+                nc.scalar.activation(
+                    out=f_scaleds[u, o][:], in_=fields[pair][:, h, :, :], func=ACT.Copy, scale=coef(o, h)
+                )
+
+        def lattice(u, q):
+            pair, h = divmod(u, H)
+            if q == 0:
+                accps[u] = ahead.tile([P, R, P], F32, name="accp", tag="accp")
+            hi = next_bank(6, 2)[:].rearrange("p (i a) -> p i a", i=4)
+            for i in range(4):
+                r = 4 * q + i
+                for o in PE_TAPS:
+                    r_src = (r - o) % R
+                    carry = (o - r + r_src) // R
+                    nc.tensor.matmul(
+                        out=hi[:, i, :], lhsT=f_scaleds[u, o][:, r_src, :],
+                        rhs=wrap[:, P - carry : 2 * P - carry], is_transpose=True,
+                        start=(o == PE_TAPS[0]), stop=False,
+                    )
+                nc.tensor.matmul(
+                    out=hi[:, i, A0:P], lhsT=fields[pair][:, h, r, :], rhs=toep[:, h, :], start=False, stop=True
+                )
+            nc.scalar.copy(out=accps[u][:, 4 * q : 4 * q + 4, A0:P], in_=hi[:, :, A0:P])
+
         with tc.tile_pool(name="once", bufs=1) as once, tc.tile_pool(name="stage", bufs=3) as stage:
             w_sb = once.tile([P, 4 * D], BF16)
-            nc.sync.dma_start(
-                out=w_sb[:, 0 : 2 * D].rearrange("p (t k) -> p t k", t=2),
-                in_=k_w.rearrange("(t p) k -> p t k", p=P),
-            )
+            for g in range(2):
+                for h in range(H):
+                    c0 = HD * h + 32 * g
+                    nc.sync.dma_start(out=w_sb[32 * h : 32 * h + 32, g * D : (g + 1) * D], in_=k_w[c0 : c0 + 32, :])
             nc.sync.dma_start(
                 out=w_sb[:, 2 * D : 4 * D].rearrange("p (t k) -> p t k", t=2),
                 in_=v_w.rearrange("(t p) k -> p t k", p=P),
             )
             kb_rows = once.tile([2, P], BF16)
-            nc.scalar.dma_start(out=kb_rows[:], in_=k_b.rearrange("(g c) -> g c", g=2))
+            nc.scalar.dma_start(
+                out=kb_rows[:].rearrange("g (h i) -> g h i", h=H), in_=k_b.rearrange("(h g i) -> g h i", h=H, g=2)
+            )
             vb_bf = once.tile([P, C], BF16)
             nc.scalar.dma_start(out=vb_bf[:], in_=v_b.partition_broadcast(P))
             sg_bf = once.tile([P, NS * H], BF16)
             nc.scalar.dma_start(out=sg_bf[:], in_=scale_gain.rearrange("j h -> (j h)").partition_broadcast(P))
             x_words = []
-            for b in range(B):
-                x_sb = once.tile([P, R * D], BF16, name="x_sb%d" % b)
+
+            def load_x(b):
+                x_sb = stage.tile([P, R * D], BF16, name="x_sb", bufs=2)
                 x_rows = x[b].rearrange("(a r) k -> a (r k)", r=R)
                 for q in range(4):
                     nc.sync.dma_start(
@@ -84,15 +121,18 @@ def tile_causalwaveletfieldattentionbyte_pa_t_kernel(tc, x, k_w, k_b, v_w, v_b, 
                     )
                 x_words.append(x_sb[:].bitcast(F32).rearrange("p (r w) -> p r w", r=R))
 
+            load_x(0)
+            load_x(1)
+
             make_identity(nc, ident[:])
-            shifts = once.tile([P, 2 * P], F32)
             nc.vector.memset(shifts[:, 0:P], 0.0)
             nc.vector.tensor_copy(out=shifts[:, P : 2 * P], in_=ident[:])
-            ind = once.tile([P, 2, H], F32)
+            nc.vector.tensor_copy(out=wrap[:, 0:P], in_=ident[:])
+            nc.vector.tensor_copy(out=wrap[:, P : 2 * P], in_=ident[:])
+            ind = once.tile([P, H], F32)
             nc.vector.memset(ind[:], 0.0)
-            for g in range(2):
-                nc.vector.memset(ind[0:64, g, 2 * g : 2 * g + 1], 1.0)
-                nc.vector.memset(ind[64:128, g, 2 * g + 1 : 2 * g + 2], 1.0)
+            for h in range(H):
+                nc.vector.memset(ind[32 * h : 32 * h + 32, h : h + 1], 1.0)
 
             w_words = w_sb[:].bitcast(F32).rearrange("p (t w) -> p t w", t=4)
             w_grp = once.tile([P, 4 * 4 * P], BF16, align_bytes=64)
@@ -141,90 +181,138 @@ def tile_causalwaveletfieldattentionbyte_pa_t_kernel(tc, x, k_w, k_b, v_w, v_b, 
             )
             nc.vector.tensor_scalar_mul(out=thr[:], in0=sg[:], scalar1=T0)
 
-            def group(b, q):
-                field = fields[b // 2]
-                b2 = b % 2
-                x_grp = stage.tile([P, 4 * TOK], BF16, align_bytes=64)
-                x_grp_words = x_grp[:].bitcast(F32).rearrange("p (t u) -> p t u", u=2)
-                for half in range(2):
-                    xt = bank((2 * q + half) % 4)[:].rearrange("p (i u a) -> p i u a", i=2, u=2)
-                    for i in range(2):
-                        for u in range(2):
-                            nc.tensor.transpose(
-                                xt[:, i, u, :], x_words[b][:, 4 * q + 2 * half + i, u * P : (u + 1) * P], ident[:]
-                            )
-                    nc.scalar.copy(
-                        out=x_grp_words[:, 2 * half * P : (2 * half + 2) * P, :].rearrange(
-                            "p (i a) u -> p i a u", i=2
-                        ),
-                        in_=xt.rearrange("p i u a -> p i a u"),
-                    )
-                x_codes = stage.tile([P, TOK], U32, align_bytes=64)
-                x_scales = stage.tile([P, TOK], U8, align_bytes=64)
-                nc.vector.quantize_mx(out=x_codes[:].bitcast(FP8X4), scales=x_scales[:], in_=x_grp[:])
+            def toeplitz_step(k):
+                for h in range(H):
+                    if k == 0:
+                        nc.vector.tensor_scalar_mul(out=toep[:, h, :], in0=shifts[:, P + A0 : 2 * P], scalar1=T3)
+                    else:
+                        s = LATTICE_STEPS[k - 1]
+                        nc.vector.scalar_tensor_tensor(
+                            out=toep[:, h, :], in0=shifts[:, P + A0 - s : 2 * P - s], scalar=coef(16 * s, h),
+                            in1=toep[:, h, :], op0=ALU.mult, op1=ALU.add,
+                        )
 
-                k_sq = stage.tile([P, 2, TOK], F32)
-                for g in range(2):
-                    k_ps = next_bank(4, 3)
+            live = {}
+
+            def transposes(n, half):
+                b, q = divmod(n, 4)
+                if half == 0:
+                    live["grp", n] = stage.tile([P, 4 * TOK], BF16, name="x_grp", align_bytes=64, bufs=2)
+                x_grp_words = live["grp", n][:].bitcast(F32).rearrange("p (t u) -> p t u", u=2)
+                xt = bank((2 * q + half) % 4)[:].rearrange("p (i u a) -> p i u a", i=2, u=2)
+                for i in range(2):
+                    for u in range(2):
+                        nc.tensor.transpose(
+                            xt[:, i, u, :], x_words[b][:, 4 * q + 2 * half + i, u * P : (u + 1) * P], ident[:]
+                        )
+                nc.scalar.copy(
+                    out=x_grp_words[:, 2 * half * P : (2 * half + 2) * P, :].rearrange("p (i a) u -> p i a u", i=2),
+                    in_=xt.rearrange("p i u a -> p i a u"),
+                )
+                if half == 1:
+                    live["codes", n] = stage.tile([P, TOK], U32, name="x_codes", align_bytes=64)
+                    live["scales", n] = stage.tile([P, TOK], U8, name="x_scales", align_bytes=64)
+                    nc.vector.quantize_mx(
+                        out=live["codes", n][:].bitcast(FP8X4), scales=live["scales", n][:], in_=live["grp", n][:]
+                    )
+
+            def project_k(n, g):
+                if g == 0:
+                    live["k_sq", n] = stage.tile([P, 2, TOK], F32, name="k_sq")
+                k_ps = next_bank(4, 3)
+                nc.tensor.matmul_mx(
+                    out=k_ps[:],
+                    lhsT=w_codes[:, g * P : (g + 1) * P].bitcast(FP8X4),
+                    lhsT_scale=w_scales[:, g * P : (g + 1) * P],
+                    rhs=live["codes", n][:].bitcast(FP8X4),
+                    rhs_scale=live["scales", n][:],
+                    start=True,
+                    stop=True,
+                )
+                nc.scalar.activation(
+                    out=live["k_sq", n][:, g, :], in_=k_ps[:], func=ACT.Square, bias=kb[:, g : g + 1], scale=1.0
+                )
+                if g == 1:
+                    nc.vector.tensor_tensor(
+                        out=live["k_sq", n][:, 0, :], in0=live["k_sq", n][:, 0, :], in1=live["k_sq", n][:, 1, :],
+                        op=ALU.add,
+                    )
+
+            def project_v(n, half):
+                if half == 0:
+                    live["v_sum", n] = stage.tile([P, 4, C], F32, name="v_sum")
+                v_ps = next_bank(4, 3)[:].rearrange("p (i c) -> p i c", i=2)
+                for i in range(2):
+                    t = 2 * half + i
                     nc.tensor.matmul_mx(
-                        out=k_ps[:],
-                        lhsT=w_codes[:, g * P : (g + 1) * P].bitcast(FP8X4),
-                        lhsT_scale=w_scales[:, g * P : (g + 1) * P],
-                        rhs=x_codes[:].bitcast(FP8X4),
-                        rhs_scale=x_scales[:],
+                        out=v_ps[:, i, :],
+                        lhsT=live["codes", n][:, t * P : (t + 1) * P].bitcast(FP8X4),
+                        lhsT_scale=live["scales", n][:, t * P : (t + 1) * P],
+                        rhs=w_codes[:, 2 * P : 4 * P].bitcast(FP8X4),
+                        rhs_scale=w_scales[:, 2 * P : 4 * P],
                         start=True,
                         stop=True,
                     )
-                    nc.scalar.activation(
-                        out=k_sq[:, g, :], in_=k_ps[:], func=ACT.Square, bias=kb[:, g : g + 1], scale=1.0
-                    )
-                m2 = bank(7)[:, 0 : 4 * H].rearrange("p (i h) -> p i h", i=4)
-                for i in range(4):
-                    for g in range(2):
-                        nc.tensor.matmul(
-                            out=m2[:, i, :], lhsT=k_sq[:, g, i * P : (i + 1) * P], rhs=ind[:, g, :],
-                            start=(g == 0), stop=(g == 1),
-                        )
-                mag = stage.tile([P, 4, H], F32)
-                nc.scalar.activation(out=mag[:], in_=m2, func=ACT.Sqrt)
+                nc.vector.tensor_tensor(
+                    out=live["v_sum", n][:, 2 * half : 2 * half + 2, :], in0=v_ps,
+                    in1=vb[:].unsqueeze(1).to_broadcast([P, 2, C]), op=ALU.add,
+                )
 
-                for half in range(2):
-                    v_ps = next_bank(4, 3)[:].rearrange("p (i c) -> p i c", i=2)
-                    for i in range(2):
-                        t = 2 * half + i
-                        nc.tensor.matmul_mx(
-                            out=v_ps[:, i, :],
-                            lhsT=x_codes[:, t * P : (t + 1) * P].bitcast(FP8X4),
-                            lhsT_scale=x_scales[:, t * P : (t + 1) * P],
-                            rhs=w_codes[:, 2 * P : 4 * P].bitcast(FP8X4),
-                            rhs_scale=w_scales[:, 2 * P : 4 * P],
-                            start=True,
-                            stop=True,
-                        )
-                    v_sum = stage.tile([P, 2, C], F32)
-                    nc.vector.tensor_tensor(
-                        out=v_sum[:], in0=v_ps, in1=vb[:].unsqueeze(1).to_broadcast([P, 2, C]), op=ALU.add
+            def norms(n, half):
+                if half == 0:
+                    live["m2", n] = bank(7)[:, 0 : 4 * H].rearrange("p (i h) -> p i h", i=4)
+                for i in range(2 * half, 2 * half + 2):
+                    nc.tensor.matmul(
+                        out=live["m2", n][:, i, :], lhsT=live["k_sq", n][:, 0, i * P : (i + 1) * P],
+                        rhs=ind[:], start=True, stop=True,
                     )
+
+            def field_product(n):
+                b, q = divmod(n, 4)
+                mag = stage.tile([P, 4, H], F32)
+                nc.scalar.activation(out=mag[:], in_=live["m2", n], func=ACT.Sqrt)
+                b2 = b % 2
+                for half in range(2):
                     r0 = 4 * q + 2 * half
                     nc.gpsimd.tensor_tensor(
-                        out=field[:, :, r0 : r0 + 2, b2 * HD : (b2 + 1) * HD].rearrange("p h i c -> p i h c"),
-                        in0=v_sum[:].rearrange("p i (h c) -> p i h c", h=H),
+                        out=fields[b // 2][:, :, r0 : r0 + 2, b2 * HD : (b2 + 1) * HD].rearrange(
+                            "p h i c -> p i h c"
+                        ),
+                        in0=live["v_sum", n][:, 2 * half : 2 * half + 2, :].rearrange("p i (h c) -> p i h c", h=H),
                         in1=mag[:, 2 * half : 2 * half + 2, :].unsqueeze(3).to_broadcast([P, 2, H, HD]),
                         op=ALU.mult,
                     )
 
-            for b in range(B):
-                for q in range(4):
-                    group(b, q)
-                if b == 0:
-                    for h in range(H):
-                        nc.vector.tensor_scalar_mul(out=toep[:, h, :], in0=shifts[:, P + A0 : 2 * P], scalar1=T3)
-                    for s in LATTICE_STEPS:
-                        for h in range(H):
-                            nc.vector.scalar_tensor_tensor(
-                                out=toep[:, h, :], in0=shifts[:, P + A0 - s : 2 * P - s], scalar=coef(16 * s, h),
-                                in1=toep[:, h, :], op0=ALU.mult, op1=ALU.add,
-                            )
+            groups = 4 * B
+            for n in range(groups + 2):
+                first, second, third = n < groups, 1 <= n <= groups, n >= 2
+                if first:
+                    transposes(n, 0)
+                if second:
+                    project_k(n - 1, 0)
+                if first:
+                    transposes(n, 1)
+                if second:
+                    project_k(n - 1, 1)
+                if third:
+                    norms(n - 2, 0)
+                if second:
+                    project_v(n - 1, 0)
+                if third:
+                    norms(n - 2, 1)
+                if second:
+                    project_v(n - 1, 1)
+                if third:
+                    field_product(n - 2)
+                if 2 <= n <= 8:
+                    toeplitz_step(2 * (n - 2))
+                    toeplitz_step(2 * (n - 2) + 1)
+                if n == 5 or n == 9:
+                    load_x(2 + (n - 5) // 4)
+                if n == 10 or n == 11:
+                    scale_field(n - 10)
+                if 12 <= n <= 15:
+                    lattice(0, n - 12)
 
         def runs(q, o):
             res = []
@@ -236,49 +324,55 @@ def tile_causalwaveletfieldattentionbyte_pa_t_kernel(tc, x, k_w, k_b, v_w, v_b, 
                     res.append((i, 1, r, carry))
             return res
 
-        head_steps = [s for s in LATTICE_STEPS if s < A0]
+        head_taps = list(PE_TAPS) + [16 * s for s in LATTICE_STEPS if s < A0]
 
         with tc.tile_pool(name="opool", bufs=2) as opool:
 
-            def unit(pair, h):
+            def scale_field_unused(u):
+                pair, h = divmod(u, H)
+                for o in PE_TAPS:
+                    f_scaleds[u, o] = opool.tile([P, R, P], F32, name="f_scaled%d" % o, tag="f_scaled%d" % o, bufs=3)
+                    nc.scalar.activation(
+                        out=f_scaleds[u, o][:], in_=fields[pair][:, h, :, :], func=ACT.Copy, scale=coef(o, h)
+                    )
+
+            def lattice_unused(u, q):
+                pair, h = divmod(u, H)
+                if q == 0:
+                    accps[u] = opool.tile([P, R, P], F32, name="accp", tag="accp", bufs=3)
+                hi = next_bank(6, 2)[:].rearrange("p (i a) -> p i a", i=4)
+                for i in range(4):
+                    r = 4 * q + i
+                    for o in PE_TAPS:
+                        r_src = (r - o) % R
+                        carry = (o - r + r_src) // R
+                        nc.tensor.matmul(
+                            out=hi[:, i, :], lhsT=f_scaleds[u, o][:, r_src, :],
+                            rhs=wrap[:, P - carry : 2 * P - carry], is_transpose=True,
+                            start=(o == PE_TAPS[0]), stop=False,
+                        )
+                    nc.tensor.matmul(
+                        out=hi[:, i, A0:P], lhsT=fields[pair][:, h, r, :], rhs=toep[:, h, :], start=False, stop=True
+                    )
+                nc.scalar.copy(out=accps[u][:, 4 * q : 4 * q + 4, A0:P], in_=hi[:, :, A0:P])
+
+            def unit(u):
+                pair, h = divmod(u, H)
                 field = fields[pair]
-                accp = opool.tile([P, R, P], F32, tag="accp", bufs=3)
+                accp = accps[u]
                 nat = opool.tile([P, N], F32, tag="nat", bufs=3)
                 nat_view = nat[:].rearrange("p (a r) -> p a r", r=R)
                 f_head = opool.tile([P, HEAD], F32, tag="f_head")
                 f_head_view = f_head[:].rearrange("p (a r) -> p a r", r=R)
-                s_head = opool.tile([P, len(head_steps), HEAD], F32, tag="s_head")
-                scaled = {}
-                for o in G_TAPS:
-                    scaled[o] = opool.tile([P, N], F32, name="scaled%d" % o, tag="scaled%d" % o)
-                for q in range(4):
-                    hi = next_bank(4, 4)[:, 0 : 4 * NHI].rearrange("p (i a) -> p i a", i=4)
-                    for i in range(4):
-                        nc.tensor.matmul(
-                            out=hi[:, i, :], lhsT=field[:, h, 4 * q + i, :], rhs=toep[:, h, :], start=True, stop=True
-                        )
-                    nc.scalar.copy(out=accp[:, 4 * q : 4 * q + 4, A0:P], in_=hi)
+                s_head = opool.tile([P, len(head_taps), HEAD], F32, tag="s_head")
                 tps = []
                 for q in range(4):
-                    tp = bank(q)[:].rearrange("p (i a) -> p i a", i=4)
+                    tp = bank((4 * u + q) % 6)[:].rearrange("p (i a) -> p i a", i=4)
                     tps.append(tp)
                     for i in range(4):
                         nc.tensor.transpose(tp[:, i, :], field[:, h, 4 * q + i, :], ident[:])
                     nc.scalar.activation(
                         out=accp[:, 4 * q : 4 * q + 4, 0:A0], in_=tp[:, :, 0:A0], func=ACT.Copy, scale=T3
-                    )
-                for q in range(4):
-                    tp_view = tps[q].rearrange("p i a -> p a i")
-                    nc.scalar.copy(out=f_head_view[:, :, 4 * q : 4 * q + 4], in_=tp_view[:, 0:A0, :])
-                    for o in G_TAPS:
-                        nc.scalar.activation(
-                            out=scaled[o][:].rearrange("p (a r) -> p a r", r=R)[:, :, 4 * q : 4 * q + 4],
-                            in_=tp_view, func=ACT.Copy, scale=coef(o, h),
-                        )
-                for k, s in enumerate(head_steps):
-                    width = HEAD - 16 * s
-                    nc.scalar.activation(
-                        out=s_head[:, k, 0:width], in_=f_head[:, 0:width], func=ACT.Copy, scale=coef(16 * s, h)
                     )
                 for o in V_TAPS:
                     for q in range(4):
@@ -304,18 +398,128 @@ def tile_causalwaveletfieldattentionbyte_pa_t_kernel(tc, x, k_w, k_b, v_w, v_b, 
                                 out=nat_view[:, 0:carry, r0 : r0 + cnt],
                                 in_=accp[:, r0 : r0 + cnt, 0:carry].rearrange("p r a -> p a r"),
                             )
-                for o in G_TAPS:
-                    nc.gpsimd.tensor_tensor(out=nat[:, o:N], in0=nat[:, o:N], in1=scaled[o][:, 0 : N - o], op=ALU.add)
-                for k, s in enumerate(head_steps):
-                    nc.gpsimd.tensor_tensor(
-                        out=nat[:, 16 * s : HEAD], in0=nat[:, 16 * s : HEAD], in1=s_head[:, k, 0 : HEAD - 16 * s],
-                        op=ALU.add,
+                for q in range(4):
+                    nc.scalar.copy(
+                        out=f_head_view[:, :, 4 * q : 4 * q + 4], in_=tps[q].rearrange("p i a -> p a i")[:, 0:A0, :]
                     )
+                share = (len(head_taps) + 2) // 3
+                for q in range(4):
+                    for k in range(q * share, min((q + 1) * share, len(head_taps))):
+                        o = head_taps[k]
+                        nc.scalar.activation(
+                            out=s_head[:, k, 0 : HEAD - o], in_=f_head[:, 0 : HEAD - o], func=ACT.Copy,
+                            scale=coef(o, h),
+                        )
+                    if q == 3 and u + 2 < UNITS:
+                        scale_field(u + 2)
+                    if u + 1 < UNITS:
+                        lattice(u + 1, q)
+                o_min = head_taps[0]
+                for k, o in enumerate(head_taps):
+                    if k > 0:
+                        nc.gpsimd.tensor_tensor(
+                            out=s_head[:, 0, o - o_min : HEAD - o_min], in0=s_head[:, 0, o - o_min : HEAD - o_min],
+                            in1=s_head[:, k, 0 : HEAD - o], op=ALU.add,
+                        )
+                nc.gpsimd.tensor_tensor(
+                    out=nat[:, o_min:HEAD], in0=nat[:, o_min:HEAD], in1=s_head[:, 0, 0 : HEAD - o_min], op=ALU.add
+                )
                 for b2 in range(2):
                     nc.sync.dma_start(
                         out=out[2 * pair + b2, h * HD : (h + 1) * HD, :], in_=nat[b2 * HD : (b2 + 1) * HD, :]
                     )
 
-            for pair in range(2):
-                for h in range(H):
-                    unit(pair, h)
+            def unit_old(u):
+                pair, h = divmod(u, H)
+                last = u == 2 * H - 1
+                v_taps = [(1, 0), (2, 0), (3, 0), (6, 0), (8, 0 if last else P // 2)]
+                g_taps = [] if last else [(8, N // 2)]
+                field = fields[pair]
+                accp = opool.tile([P, R, P], F32, tag="accp", bufs=3)
+                nat = opool.tile([P, N], F32, tag="nat", bufs=3)
+                nat_view = nat[:].rearrange("p (a r) -> p a r", r=R)
+                f_head = opool.tile([P, HEAD], F32, tag="f_head")
+                f_head_view = f_head[:].rearrange("p (a r) -> p a r", r=R)
+                s_head = opool.tile([P, len(head_taps), HEAD], F32, tag="s_head")
+                scaled = {}
+                for o, up in g_taps:
+                    scaled[o] = opool.tile([P, up], F32, name="scaled%d" % o, tag="scaled%d" % o)
+                f_scaled = {}
+                for o in PE_TAPS:
+                    f_scaled[o] = opool.tile([P, R, P], F32, name="f_scaled%d" % o, tag="f_scaled%d" % o)
+                    nc.scalar.activation(out=f_scaled[o][:], in_=field[:, h, :, :], func=ACT.Copy, scale=coef(o, h))
+                for q in range(4):
+                    hi = next_bank(6, 2)[:].rearrange("p (i a) -> p i a", i=4)
+                    for i in range(4):
+                        r = 4 * q + i
+                        for o in PE_TAPS:
+                            r_src = (r - o) % R
+                            carry = (o - r + r_src) // R
+                            nc.tensor.matmul(
+                                out=hi[:, i, :], lhsT=f_scaled[o][:, r_src, :],
+                                rhs=wrap[:, P - carry : 2 * P - carry], is_transpose=True,
+                                start=(o == PE_TAPS[0]), stop=False,
+                            )
+                        nc.tensor.matmul(
+                            out=hi[:, i, A0:P], lhsT=field[:, h, r, :], rhs=toep[:, h, :], start=False, stop=True
+                        )
+                    nc.scalar.copy(out=accp[:, 4 * q : 4 * q + 4, A0:P], in_=hi[:, :, A0:P])
+                tps = []
+                for q in range(4):
+                    tp = bank((4 * u + q) % 6)[:].rearrange("p (i a) -> p i a", i=4)
+                    tps.append(tp)
+                    for i in range(4):
+                        nc.tensor.transpose(tp[:, i, :], field[:, h, 4 * q + i, :], ident[:])
+                    nc.scalar.activation(
+                        out=accp[:, 4 * q : 4 * q + 4, 0:A0], in_=tp[:, :, 0:A0], func=ACT.Copy, scale=T3
+                    )
+                for q in range(4):
+                    tp_view = tps[q].rearrange("p i a -> p a i")
+                    nc.scalar.copy(out=f_head_view[:, :, 4 * q : 4 * q + 4], in_=tp_view[:, 0:A0, :])
+                    for o, up in g_taps:
+                        nc.scalar.activation(
+                            out=scaled[o][:].rearrange("p (a r) -> p a r", r=R)[:, :, 4 * q : 4 * q + 4],
+                            in_=tp_view[:, 0 : up // R, :], func=ACT.Copy, scale=coef(o, h),
+                        )
+                for k, o in enumerate(head_taps):
+                    nc.scalar.activation(
+                        out=s_head[:, k, 0 : HEAD - o], in_=f_head[:, 0 : HEAD - o], func=ACT.Copy, scale=coef(o, h)
+                    )
+                for o, a_lo in v_taps:
+                    for q in range(4):
+                        for i0, cnt, r0, carry in runs(q, o):
+                            lo = max(a_lo, carry)
+                            nc.vector.scalar_tensor_tensor(
+                                out=accp[:, r0 : r0 + cnt, lo:P],
+                                in0=tps[q][:, i0 : i0 + cnt, lo - carry : P - carry],
+                                scalar=coef(o, h),
+                                in1=accp[:, r0 : r0 + cnt, lo:P],
+                                op0=ALU.mult, op1=ALU.add,
+                            )
+                for q in range(4):
+                    for i0, cnt, r0, carry in runs(q, LAST_TAP):
+                        nc.vector.scalar_tensor_tensor(
+                            out=nat_view[:, carry:P, r0 : r0 + cnt],
+                            in0=tps[q][:, i0 : i0 + cnt, 0 : P - carry].rearrange("p i a -> p a i"),
+                            scalar=coef(LAST_TAP, h),
+                            in1=accp[:, r0 : r0 + cnt, carry:P].rearrange("p r a -> p a r"),
+                            op0=ALU.mult, op1=ALU.add,
+                        )
+                        if carry:
+                            nc.vector.tensor_copy(
+                                out=nat_view[:, 0:carry, r0 : r0 + cnt],
+                                in_=accp[:, r0 : r0 + cnt, 0:carry].rearrange("p r a -> p a r"),
+                            )
+                for k, o in enumerate(head_taps):
+                    nc.gpsimd.tensor_tensor(
+                        out=nat[:, o:HEAD], in0=nat[:, o:HEAD], in1=s_head[:, k, 0 : HEAD - o], op=ALU.add
+                    )
+                for o, up in g_taps:
+                    nc.gpsimd.tensor_tensor(out=nat[:, o:up], in0=nat[:, o:up], in1=scaled[o][:, 0 : up - o], op=ALU.add)
+                for b2 in range(2):
+                    nc.sync.dma_start(
+                        out=out[2 * pair + b2, h * HD : (h + 1) * HD, :], in_=nat[b2 * HD : (b2 + 1) * HD, :]
+                    )
+
+            for u in range(UNITS):
+                unit(u)

@@ -34,6 +34,7 @@ FLOPS = 2 * B * N * D * 2 * C
 def tile_causalwaveletfieldattentionbyte_pa_t_kernel(tc, x, k_w, k_b, v_w, v_b, scale_gain, out):
     nc = tc.nc
     with ExitStack() as ctx:
+        ctx.enter_context(tc.manual_schedule())
         const = ctx.enter_context(tc.tile_pool(name="const", bufs=1))
         psum = ctx.enter_context(tc.psum_pool(name="psum", bufs=1))
         turn = [0]

@@ -19,7 +19,7 @@ R = N // P
 TOK = 4 * P
 BANK = 512
 T0, T1, T2, T3 = 0.4829629131445341, 0.8365163037378079, 0.2241438680420134, -0.1294095225512604
-A0 = 32
+A0 = 28
 NHI = P - A0
 HEAD = 16 * A0
 LATTICE_STEPS = (1, 2, 3, 4, 6, 8, 12, 16, 24, 32, 48, 64, 96)
@@ -34,7 +34,6 @@ FLOPS = 2 * B * N * D * 2 * C
 def tile_causalwaveletfieldattentionbyte_pa_t_kernel(tc, x, k_w, k_b, v_w, v_b, scale_gain, out):
     nc = tc.nc
     with ExitStack() as ctx:
-        ctx.enter_context(tc.manual_schedule())
         const = ctx.enter_context(tc.tile_pool(name="const", bufs=1))
         psum = ctx.enter_context(tc.psum_pool(name="psum", bufs=1))
         turn = [0]
@@ -200,7 +199,7 @@ def tile_causalwaveletfieldattentionbyte_pa_t_kernel(tc, x, k_w, k_b, v_w, v_b, 
                 if half == 0:
                     live["grp", n] = stage.tile([P, 4 * TOK], BF16, name="x_grp", align_bytes=64, bufs=2)
                 x_grp_words = live["grp", n][:].bitcast(F32).rearrange("p (t u) -> p t u", u=2)
-                xt = bank((2 * q + half) % 4)[:].rearrange("p (i u a) -> p i u a", i=2, u=2)
+                xt = bank((2 * n + half) % 3)[:].rearrange("p (i u a) -> p i u a", i=2, u=2)
                 for i in range(2):
                     for u in range(2):
                         nc.tensor.transpose(
@@ -261,7 +260,7 @@ def tile_causalwaveletfieldattentionbyte_pa_t_kernel(tc, x, k_w, k_b, v_w, v_b, 
 
             def norms(n, half):
                 if half == 0:
-                    live["m2", n] = bank(7)[:, 0 : 4 * H].rearrange("p (i h) -> p i h", i=4)
+                    live["m2", n] = bank(3 + 4 * (n % 2))[:, 0 : 4 * H].rearrange("p (i h) -> p i h", i=4)
                 for i in range(2 * half, 2 * half + 2):
                     nc.tensor.matmul(
                         out=live["m2", n][:, i, :], lhsT=live["k_sq", n][:, 0, i * P : (i + 1) * P],

@@ -364,7 +364,8 @@ def tile_causalwaveletfieldattentionbyte_pa_t_kernel(tc, x, k_w, k_b, v_w, v_b, 
                 nat_view = nat[:].rearrange("p (a r) -> p a r", r=R)
                 f_head = opool.tile([P, HEAD], F32, tag="f_head")
                 f_head_view = f_head[:].rearrange("p (a r) -> p a r", r=R)
-                s_head = opool.tile([P, len(head_taps), HEAD], F32, tag="s_head")
+                last = u == UNITS - 1
+                s_head = None if last else opool.tile([P, len(head_taps), HEAD], F32, name="s_head", tag="s_head")
                 tps = []
                 for q in range(4):
                     tp = bank((4 * u + q) % 6)[:].rearrange("p (i a) -> p i a", i=4)
@@ -404,7 +405,7 @@ def tile_causalwaveletfieldattentionbyte_pa_t_kernel(tc, x, k_w, k_b, v_w, v_b, 
                     )
                 share = (len(head_taps) + 2) // 3
                 for q in range(4):
-                    for k in range(q * share, min((q + 1) * share, len(head_taps))):
+                    for k in range(q * share, 0 if last else min((q + 1) * share, len(head_taps))):
                         o = head_taps[k]
                         nc.scalar.activation(
                             out=s_head[:, k, 0 : HEAD - o], in_=f_head[:, 0 : HEAD - o], func=ACT.Copy,
@@ -415,15 +416,24 @@ def tile_causalwaveletfieldattentionbyte_pa_t_kernel(tc, x, k_w, k_b, v_w, v_b, 
                     if u + 1 < UNITS:
                         lattice(u + 1, q)
                 o_min = head_taps[0]
+                if last:
+                    for o in head_taps:
+                        for lo, up in ((0, HEAD // 2), (HEAD // 2, HEAD)):
+                            if o < up:
+                                nc.vector.scalar_tensor_tensor(
+                                    out=nat[:, max(o, lo) : up], in0=f_head[:, max(o, lo) - o : up - o],
+                                    scalar=coef(o, h), in1=nat[:, max(o, lo) : up], op0=ALU.mult, op1=ALU.add,
+                                )
                 for k, o in enumerate(head_taps):
-                    if k > 0:
+                    if k > 0 and not last:
                         nc.gpsimd.tensor_tensor(
                             out=s_head[:, 0, o - o_min : HEAD - o_min], in0=s_head[:, 0, o - o_min : HEAD - o_min],
                             in1=s_head[:, k, 0 : HEAD - o], op=ALU.add,
                         )
-                nc.gpsimd.tensor_tensor(
-                    out=nat[:, o_min:HEAD], in0=nat[:, o_min:HEAD], in1=s_head[:, 0, 0 : HEAD - o_min], op=ALU.add
-                )
+                if not last:
+                    nc.gpsimd.tensor_tensor(
+                        out=nat[:, o_min:HEAD], in0=nat[:, o_min:HEAD], in1=s_head[:, 0, 0 : HEAD - o_min], op=ALU.add
+                    )
                 for b2 in range(2):
                     nc.sync.dma_start(
                         out=out[2 * pair + b2, h * HD : (h + 1) * HD, :], in_=nat[b2 * HD : (b2 + 1) * HD, :]

from contextlib import ExitStack

import concourse.mybir as mybir
from concourse.masks import make_identity

F32 = mybir.dt.float32
BF16 = mybir.dt.bfloat16
U32 = mybir.dt.uint32
U8 = mybir.dt.uint8
FP8X4 = mybir.dt.float8_e4m3fn_x4
ALU = mybir.AluOpType
ACT = mybir.ActivationFunctionType
AX = mybir.AxisListType

P = 128
B, N, D, C, H, NS = 4, 2048, 512, 256, 4, 11
HD = C // H
R = N // P
TOK = 4 * P
BANK = 512
T0, T1, T2, T3 = 0.4829629131445341, 0.8365163037378079, 0.2241438680420134, -0.1294095225512604
A0 = 28
NHI = P - A0
HEAD = 16 * A0
LATTICE_STEPS = (1, 2, 3, 4, 6, 8, 12, 16, 24, 32, 48, 64, 96)
PE_TAPS = (12, 24)
V_TAPS = (1, 2, 3, 6, 8)
LAST_TAP = 4
UNITS = 2 * H

FLOPS = 2 * B * N * D * 2 * C


def tile_causalwaveletfieldattentionbyte_pa_t_kernel(tc, x, k_w, k_b, v_w, v_b, scale_gain, out):
    nc = tc.nc
    with ExitStack() as ctx:
        const = ctx.enter_context(tc.tile_pool(name="const", bufs=1))
        psum = ctx.enter_context(tc.psum_pool(name="psum", bufs=1))
        turn = [0]

        def bank(k):
            return psum.tile([P, BANK], F32, name="bank%d" % k, tag="bank%d" % k)

        def next_bank(first, count):
            turn[0] += 1
            return bank(first + turn[0] % count)

        fields = [const.tile([P, H, R, P], F32, name="field%d" % pair) for pair in range(2)]
        ident = const.tile([P, P], F32)
        shifts = const.tile([P, 2 * P], F32)
        wrap = const.tile([P, 2 * P], F32)
        pow2 = const.tile([P, H, NS], F32)
        thr = const.tile([P, H, NS], F32)
        toep = const.tile([P, H, NHI], F32)

        def coef(offset, h):
            for j in range(NS):
                if offset == 2**j:
                    return pow2[:, h, j : j + 1]
                if offset == 3 * 2**j:
                    return thr[:, h, j : j + 1]
            raise ValueError("no such tap")

        ahead = ctx.enter_context(tc.tile_pool(name="ahead", bufs=3))
        accps, f_scaleds = {}, {}

        def scale_field(u):
            pair, h = divmod(u, H)
            for o in PE_TAPS:
                f_scaleds[u, o] = ahead.tile([P, R, P], F32, name="f_scaled%d" % o, tag="f_scaled%d" % o)
                nc.scalar.activation(
                    out=f_scaleds[u, o][:], in_=fields[pair][:, h, :, :], func=ACT.Copy, scale=coef(o, h)
                )

        def lattice(u, q):
            pair, h = divmod(u, H)
            if q == 0:
                accps[u] = ahead.tile([P, R, P], F32, name="accp", tag="accp")
            hi = next_bank(6, 2)[:].rearrange("p (i a) -> p i a", i=4)
            for i in range(4):
                r = 4 * q + i
                for o in PE_TAPS:
                    r_src = (r - o) % R
                    carry = (o - r + r_src) // R
                    nc.tensor.matmul(
                        out=hi[:, i, :], lhsT=f_scaleds[u, o][:, r_src, :],
                        rhs=wrap[:, P - carry : 2 * P - carry], is_transpose=True,
                        start=(o == PE_TAPS[0]), stop=False,
                    )
                nc.tensor.matmul(
                    out=hi[:, i, A0:P], lhsT=fields[pair][:, h, r, :], rhs=toep[:, h, :], start=False, stop=True
                )
            nc.scalar.copy(out=accps[u][:, 4 * q : 4 * q + 4, A0:P], in_=hi[:, :, A0:P])

        with tc.tile_pool(name="once", bufs=1) as once, tc.tile_pool(name="stage", bufs=3) as stage:
            w_sb = once.tile([P, 4 * D], BF16)
            for g in range(2):
                for h in range(H):
                    c0 = HD * h + 32 * g
                    nc.sync.dma_start(out=w_sb[32 * h : 32 * h + 32, g * D : (g + 1) * D], in_=k_w[c0 : c0 + 32, :])
            nc.sync.dma_start(
                out=w_sb[:, 2 * D : 4 * D].rearrange("p (t k) -> p t k", t=2),
                in_=v_w.rearrange("(t p) k -> p t k", p=P),
            )
            kb_rows = once.tile([2, P], BF16)
            nc.scalar.dma_start(
                out=kb_rows[:].rearrange("g (h i) -> g h i", h=H), in_=k_b.rearrange("(h g i) -> g h i", h=H, g=2)
            )
            vb_bf = once.tile([P, C], BF16)
            nc.scalar.dma_start(out=vb_bf[:], in_=v_b.partition_broadcast(P))
            sg_bf = once.tile([P, NS * H], BF16)
            nc.scalar.dma_start(out=sg_bf[:], in_=scale_gain.rearrange("j h -> (j h)").partition_broadcast(P))
            x_words = []

            def load_x(b):
                x_sb = stage.tile([P, R * D], BF16, name="x_sb", bufs=2)
                x_rows = x[b].rearrange("(a r) k -> a (r k)", r=R)
                for q in range(4):
                    nc.sync.dma_start(
                        out=x_sb[:, q * 4 * D : (q + 1) * 4 * D], in_=x_rows[:, q * 4 * D : (q + 1) * 4 * D]
                    )
                x_words.append(x_sb[:].bitcast(F32).rearrange("p (r w) -> p r w", r=R))

            load_x(0)
            load_x(1)

            make_identity(nc, ident[:])
            nc.vector.memset(shifts[:, 0:P], 0.0)
            nc.vector.tensor_copy(out=shifts[:, P : 2 * P], in_=ident[:])
            nc.vector.tensor_copy(out=wrap[:, 0:P], in_=ident[:])
            nc.vector.tensor_copy(out=wrap[:, P : 2 * P], in_=ident[:])
            ind = once.tile([P, H], F32)
            nc.vector.memset(ind[:], 0.0)
            for h in range(H):
                nc.vector.memset(ind[32 * h : 32 * h + 32, h : h + 1], 1.0)

            w_words = w_sb[:].bitcast(F32).rearrange("p (t w) -> p t w", t=4)
            w_grp = once.tile([P, 4 * 4 * P], BF16, align_bytes=64)
            w_grp_words = w_grp[:].bitcast(F32).rearrange("p (c u) -> p c u", u=2)
            for half in range(2):
                wt = bank(half)[:].rearrange("p (i u c) -> p i u c", i=2, u=2)
                for i in range(2):
                    for u in range(2):
                        nc.tensor.transpose(wt[:, i, u, :], w_words[:, 2 * half + i, u * P : (u + 1) * P], ident[:])
                nc.vector.tensor_copy(
                    out=w_grp_words[:, 2 * half * P : (2 * half + 2) * P, :].rearrange("p (i c) u -> p i c u", i=2),
                    in_=wt.rearrange("p i u c -> p i c u"),
                )
            w_codes = once.tile([P, 4 * P], U32, align_bytes=64)
            w_scales = once.tile([P, 4 * P], U8, align_bytes=64)
            nc.vector.quantize_mx(out=w_codes[:].bitcast(FP8X4), scales=w_scales[:], in_=w_grp[:])

            kb_pad = once.tile([P, P], F32)
            nc.vector.memset(kb_pad[:], 0.0)
            nc.vector.tensor_copy(out=kb_pad[0:2, :], in_=kb_rows[:])
            kb_ps = bank(2)
            nc.tensor.transpose(kb_ps[:, 0:P], kb_pad[:], ident[:])
            kb = once.tile([P, 2], F32)
            nc.vector.tensor_copy(out=kb[:], in_=kb_ps[:, 0:2])
            vb = once.tile([P, C], F32)
            nc.vector.tensor_copy(out=vb[:], in_=vb_bf[:])

            sg = once.tile([P, H, NS], F32)
            nc.vector.tensor_copy(out=sg[:], in_=sg_bf[:].rearrange("p (j h) -> p h j", h=H))
            top = once.tile([P, H], F32)
            nc.vector.tensor_reduce(out=top[:], in_=sg[:], axis=AX.X, op=ALU.max)
            nc.vector.tensor_tensor(
                out=sg[:], in0=sg[:], in1=top[:].unsqueeze(2).to_broadcast([P, H, NS]), op=ALU.subtract
            )
            nc.scalar.activation(out=sg[:], in_=sg[:], func=ACT.Exp)
            tot = once.tile([P, H], F32)
            nc.vector.tensor_reduce(out=tot[:], in_=sg[:], axis=AX.X, op=ALU.add)
            nc.vector.reciprocal(out=tot[:], in_=tot[:])
            nc.vector.tensor_tensor(
                out=sg[:], in0=sg[:], in1=tot[:].unsqueeze(2).to_broadcast([P, H, NS]), op=ALU.mult
            )
            nc.vector.tensor_scalar_mul(out=pow2[:], in0=sg[:], scalar1=T2)
            nc.vector.scalar_tensor_tensor(
                out=pow2[:, :, 1:NS], in0=sg[:, :, 0 : NS - 1], scalar=T1, in1=pow2[:, :, 1:NS],
                op0=ALU.mult, op1=ALU.add,
            )
            nc.vector.tensor_scalar_mul(out=thr[:], in0=sg[:], scalar1=T0)

            def toeplitz_step(k):
                for h in range(H):
                    if k == 0:
                        nc.vector.tensor_scalar_mul(out=toep[:, h, :], in0=shifts[:, P + A0 : 2 * P], scalar1=T3)
                    else:
                        s = LATTICE_STEPS[k - 1]
                        nc.vector.scalar_tensor_tensor(
                            out=toep[:, h, :], in0=shifts[:, P + A0 - s : 2 * P - s], scalar=coef(16 * s, h),
                            in1=toep[:, h, :], op0=ALU.mult, op1=ALU.add,
                        )

            live = {}

            def transposes(n, half):
                b, q = divmod(n, 4)
                if half == 0:
                    live["grp", n] = stage.tile([P, 4 * TOK], BF16, name="x_grp", align_bytes=64, bufs=2)
                x_grp_words = live["grp", n][:].bitcast(F32).rearrange("p (t u) -> p t u", u=2)
                xt = bank((2 * n + half) % 3)[:].rearrange("p (i u a) -> p i u a", i=2, u=2)
                for i in range(2):
                    for u in range(2):
                        nc.tensor.transpose(
                            xt[:, i, u, :], x_words[b][:, 4 * q + 2 * half + i, u * P : (u + 1) * P], ident[:]
                        )
                nc.scalar.copy(
                    out=x_grp_words[:, 2 * half * P : (2 * half + 2) * P, :].rearrange("p (i a) u -> p i a u", i=2),
                    in_=xt.rearrange("p i u a -> p i a u"),
                )
                if half == 1:
                    live["codes", n] = stage.tile([P, TOK], U32, name="x_codes", align_bytes=64)
                    live["scales", n] = stage.tile([P, TOK], U8, name="x_scales", align_bytes=64)
                    nc.vector.quantize_mx(
                        out=live["codes", n][:].bitcast(FP8X4), scales=live["scales", n][:], in_=live["grp", n][:]
                    )

            def project_k(n, g):
                if g == 0:
                    live["k_sq", n] = stage.tile([P, 2, TOK], F32, name="k_sq")
                k_ps = next_bank(4, 3)
                nc.tensor.matmul_mx(
                    out=k_ps[:],
                    lhsT=w_codes[:, g * P : (g + 1) * P].bitcast(FP8X4),
                    lhsT_scale=w_scales[:, g * P : (g + 1) * P],
                    rhs=live["codes", n][:].bitcast(FP8X4),
                    rhs_scale=live["scales", n][:],
                    start=True,
                    stop=True,
                )
                nc.scalar.activation(
                    out=live["k_sq", n][:, g, :], in_=k_ps[:], func=ACT.Square, bias=kb[:, g : g + 1], scale=1.0
                )
                if g == 1:
                    nc.vector.tensor_tensor(
                        out=live["k_sq", n][:, 0, :], in0=live["k_sq", n][:, 0, :], in1=live["k_sq", n][:, 1, :],
                        op=ALU.add,
                    )

            def project_v(n, half):
                if half == 0:
                    live["v_sum", n] = stage.tile([P, 4, C], F32, name="v_sum")
                v_ps = next_bank(4, 3)[:].rearrange("p (i c) -> p i c", i=2)
                for i in range(2):
                    t = 2 * half + i
                    nc.tensor.matmul_mx(
                        out=v_ps[:, i, :],
                        lhsT=live["codes", n][:, t * P : (t + 1) * P].bitcast(FP8X4),
                        lhsT_scale=live["scales", n][:, t * P : (t + 1) * P],
                        rhs=w_codes[:, 2 * P : 4 * P].bitcast(FP8X4),
                        rhs_scale=w_scales[:, 2 * P : 4 * P],
                        start=True,
                        stop=True,
                    )
                nc.vector.tensor_tensor(
                    out=live["v_sum", n][:, 2 * half : 2 * half + 2, :], in0=v_ps,
                    in1=vb[:].unsqueeze(1).to_broadcast([P, 2, C]), op=ALU.add,
                )

            def norms(n, half):
                if half == 0:
                    live["m2", n] = bank(3 + 4 * (n % 2))[:, 0 : 4 * H].rearrange("p (i h) -> p i h", i=4)
                for i in range(2 * half, 2 * half + 2):
                    nc.tensor.matmul(
                        out=live["m2", n][:, i, :], lhsT=live["k_sq", n][:, 0, i * P : (i + 1) * P],
                        rhs=ind[:], start=True, stop=True,
                    )

            def field_product(n):
                b, q = divmod(n, 4)
                mag = stage.tile([P, 4, H], F32)
                nc.scalar.activation(out=mag[:], in_=live["m2", n], func=ACT.Sqrt)
                b2 = b % 2
                for half in range(2):
                    r0 = 4 * q + 2 * half
                    nc.gpsimd.tensor_tensor(
                        out=fields[b // 2][:, :, r0 : r0 + 2, b2 * HD : (b2 + 1) * HD].rearrange(
                            "p h i c -> p i h c"
                        ),
                        in0=live["v_sum", n][:, 2 * half : 2 * half + 2, :].rearrange("p i (h c) -> p i h c", h=H),
                        in1=mag[:, 2 * half : 2 * half + 2, :].unsqueeze(3).to_broadcast([P, 2, H, HD]),
                        op=ALU.mult,
                    )

            groups = 4 * B
            for n in range(groups + 2):
                first, second, third = n < groups, 1 <= n <= groups, n >= 2
                if first:
                    transposes(n, 0)
                if second:
                    project_k(n - 1, 0)
                if first:
                    transposes(n, 1)
                if second:
                    project_k(n - 1, 1)
                if third:
                    norms(n - 2, 0)
                if second:
                    project_v(n - 1, 0)
                if third:
                    norms(n - 2, 1)
                if second:
                    project_v(n - 1, 1)
                if third:
                    field_product(n - 2)
                if 2 <= n <= 8:
                    toeplitz_step(2 * (n - 2))
                    toeplitz_step(2 * (n - 2) + 1)
                if n == 5 or n == 9:
                    load_x(2 + (n - 5) // 4)
                if n == 10 or n == 11:
                    scale_field(n - 10)
                if 12 <= n <= 15:
                    lattice(0, n - 12)

        def runs(q, o):
            res = []
            for i in range(4):
                carry, r = divmod(4 * q + i + o, R)
                if res and res[-1][3] == carry:
                    res[-1] = (res[-1][0], res[-1][1] + 1, res[-1][2], carry)
                else:
                    res.append((i, 1, r, carry))
            return res

        head_taps = list(PE_TAPS) + [16 * s for s in LATTICE_STEPS if s < A0]

        with tc.tile_pool(name="opool", bufs=2) as opool:

            def scale_field_unused(u):
                pair, h = divmod(u, H)
                for o in PE_TAPS:
                    f_scaleds[u, o] = opool.tile([P, R, P], F32, name="f_scaled%d" % o, tag="f_scaled%d" % o, bufs=3)
                    nc.scalar.activation(
                        out=f_scaleds[u, o][:], in_=fields[pair][:, h, :, :], func=ACT.Copy, scale=coef(o, h)
                    )

            def lattice_unused(u, q):
                pair, h = divmod(u, H)
                if q == 0:
                    accps[u] = opool.tile([P, R, P], F32, name="accp", tag="accp", bufs=3)
                hi = next_bank(6, 2)[:].rearrange("p (i a) -> p i a", i=4)
                for i in range(4):
                    r = 4 * q + i
                    for o in PE_TAPS:
                        r_src = (r - o) % R
                        carry = (o - r + r_src) // R
                        nc.tensor.matmul(
                            out=hi[:, i, :], lhsT=f_scaleds[u, o][:, r_src, :],
                            rhs=wrap[:, P - carry : 2 * P - carry], is_transpose=True,
                            start=(o == PE_TAPS[0]), stop=False,
                        )
                    nc.tensor.matmul(
                        out=hi[:, i, A0:P], lhsT=fields[pair][:, h, r, :], rhs=toep[:, h, :], start=False, stop=True
                    )
                nc.scalar.copy(out=accps[u][:, 4 * q : 4 * q + 4, A0:P], in_=hi[:, :, A0:P])

            def unit(u):
                pair, h = divmod(u, H)
                field = fields[pair]
                accp = accps[u]
                nat = opool.tile([P, N], F32, tag="nat", bufs=3)
                nat_view = nat[:].rearrange("p (a r) -> p a r", r=R)
                f_head = opool.tile([P, HEAD], F32, tag="f_head")
                f_head_view = f_head[:].rearrange("p (a r) -> p a r", r=R)
                last = u == UNITS - 1
                s_head = None if last else opool.tile([P, len(head_taps), HEAD], F32, name="s_head", tag="s_head")
                tps = []
                for q in range(4):
                    tp = bank((4 * u + q) % 6)[:].rearrange("p (i a) -> p i a", i=4)
                    tps.append(tp)
                    for i in range(4):
                        nc.tensor.transpose(tp[:, i, :], field[:, h, 4 * q + i, :], ident[:])
                    nc.scalar.activation(
                        out=accp[:, 4 * q : 4 * q + 4, 0:A0], in_=tp[:, :, 0:A0], func=ACT.Copy, scale=T3
                    )
                for o in V_TAPS:
                    for q in range(4):
                        for i0, cnt, r0, carry in runs(q, o):
                            nc.vector.scalar_tensor_tensor(
                                out=accp[:, r0 : r0 + cnt, carry:P],
                                in0=tps[q][:, i0 : i0 + cnt, 0 : P - carry],
                                scalar=coef(o, h),
                                in1=accp[:, r0 : r0 + cnt, carry:P],
                                op0=ALU.mult, op1=ALU.add,
                            )
                for q in range(4):
                    for i0, cnt, r0, carry in runs(q, LAST_TAP):
                        nc.vector.scalar_tensor_tensor(
                            out=nat_view[:, carry:P, r0 : r0 + cnt],
                            in0=tps[q][:, i0 : i0 + cnt, 0 : P - carry].rearrange("p i a -> p a i"),
                            scalar=coef(LAST_TAP, h),
                            in1=accp[:, r0 : r0 + cnt, carry:P].rearrange("p r a -> p a r"),
                            op0=ALU.mult, op1=ALU.add,
                        )
                        if carry:
                            nc.vector.tensor_copy(
                                out=nat_view[:, 0:carry, r0 : r0 + cnt],
                                in_=accp[:, r0 : r0 + cnt, 0:carry].rearrange("p r a -> p a r"),
                            )
                for q in range(4):
                    nc.scalar.copy(
                        out=f_head_view[:, :, 4 * q : 4 * q + 4], in_=tps[q].rearrange("p i a -> p a i")[:, 0:A0, :]
                    )
                share = (len(head_taps) + 2) // 3
                for q in range(4):
                    for k in range(q * share, 0 if last else min((q + 1) * share, len(head_taps))):
                        o = head_taps[k]
                        nc.scalar.activation(
                            out=s_head[:, k, 0 : HEAD - o], in_=f_head[:, 0 : HEAD - o], func=ACT.Copy,
                            scale=coef(o, h),
                        )
                    if q == 3 and u + 2 < UNITS:
                        scale_field(u + 2)
                    if u + 1 < UNITS:
                        lattice(u + 1, q)
                o_min = head_taps[0]
                if last:
                    for o in head_taps:
                        for lo, up in ((0, HEAD // 2), (HEAD // 2, HEAD)):
                            if o < up:
                                nc.vector.scalar_tensor_tensor(
                                    out=nat[:, max(o, lo) : up], in0=f_head[:, max(o, lo) - o : up - o],
                                    scalar=coef(o, h), in1=nat[:, max(o, lo) : up], op0=ALU.mult, op1=ALU.add,
                                )
                for k, o in enumerate(head_taps):
                    if k > 0 and not last:
                        nc.gpsimd.tensor_tensor(
                            out=s_head[:, 0, o - o_min : HEAD - o_min], in0=s_head[:, 0, o - o_min : HEAD - o_min],
                            in1=s_head[:, k, 0 : HEAD - o], op=ALU.add,
                        )
                if not last:
                    nc.gpsimd.tensor_tensor(
                        out=nat[:, o_min:HEAD], in0=nat[:, o_min:HEAD], in1=s_head[:, 0, 0 : HEAD - o_min], op=ALU.add
                    )
                for b2 in range(2):
                    nc.sync.dma_start(
                        out=out[2 * pair + b2, h * HD : (h + 1) * HD, :], in_=nat[b2 * HD : (b2 + 1) * HD, :]
                    )

            def unit_old(u):
                pair, h = divmod(u, H)
                last = u == 2 * H - 1
                v_taps = [(1, 0), (2, 0), (3, 0), (6, 0), (8, 0 if last else P // 2)]
                g_taps = [] if last else [(8, N // 2)]
                field = fields[pair]
                accp = opool.tile([P, R, P], F32, tag="accp", bufs=3)
                nat = opool.tile([P, N], F32, tag="nat", bufs=3)
                nat_view = nat[:].rearrange("p (a r) -> p a r", r=R)
                f_head = opool.tile([P, HEAD], F32, tag="f_head")
                f_head_view = f_head[:].rearrange("p (a r) -> p a r", r=R)
                s_head = opool.tile([P, len(head_taps), HEAD], F32, tag="s_head")
                scaled = {}
                for o, up in g_taps:
                    scaled[o] = opool.tile([P, up], F32, name="scaled%d" % o, tag="scaled%d" % o)
                f_scaled = {}
                for o in PE_TAPS:
                    f_scaled[o] = opool.tile([P, R, P], F32, name="f_scaled%d" % o, tag="f_scaled%d" % o)
                    nc.scalar.activation(out=f_scaled[o][:], in_=field[:, h, :, :], func=ACT.Copy, scale=coef(o, h))
                for q in range(4):
                    hi = next_bank(6, 2)[:].rearrange("p (i a) -> p i a", i=4)
                    for i in range(4):
                        r = 4 * q + i
                        for o in PE_TAPS:
                            r_src = (r - o) % R
                            carry = (o - r + r_src) // R
                            nc.tensor.matmul(
                                out=hi[:, i, :], lhsT=f_scaled[o][:, r_src, :],
                                rhs=wrap[:, P - carry : 2 * P - carry], is_transpose=True,
                                start=(o == PE_TAPS[0]), stop=False,
                            )
                        nc.tensor.matmul(
                            out=hi[:, i, A0:P], lhsT=field[:, h, r, :], rhs=toep[:, h, :], start=False, stop=True
                        )
                    nc.scalar.copy(out=accp[:, 4 * q : 4 * q + 4, A0:P], in_=hi[:, :, A0:P])
                tps = []
                for q in range(4):
                    tp = bank((4 * u + q) % 6)[:].rearrange("p (i a) -> p i a", i=4)
                    tps.append(tp)
                    for i in range(4):
                        nc.tensor.transpose(tp[:, i, :], field[:, h, 4 * q + i, :], ident[:])
                    nc.scalar.activation(
                        out=accp[:, 4 * q : 4 * q + 4, 0:A0], in_=tp[:, :, 0:A0], func=ACT.Copy, scale=T3
                    )
                for q in range(4):
                    tp_view = tps[q].rearrange("p i a -> p a i")
                    nc.scalar.copy(out=f_head_view[:, :, 4 * q : 4 * q + 4], in_=tp_view[:, 0:A0, :])
                    for o, up in g_taps:
                        nc.scalar.activation(
                            out=scaled[o][:].rearrange("p (a r) -> p a r", r=R)[:, :, 4 * q : 4 * q + 4],
                            in_=tp_view[:, 0 : up // R, :], func=ACT.Copy, scale=coef(o, h),
                        )
                for k, o in enumerate(head_taps):
                    nc.scalar.activation(
                        out=s_head[:, k, 0 : HEAD - o], in_=f_head[:, 0 : HEAD - o], func=ACT.Copy, scale=coef(o, h)
                    )
                for o, a_lo in v_taps:
                    for q in range(4):
                        for i0, cnt, r0, carry in runs(q, o):
                            lo = max(a_lo, carry)
                            nc.vector.scalar_tensor_tensor(
                                out=accp[:, r0 : r0 + cnt, lo:P],
                                in0=tps[q][:, i0 : i0 + cnt, lo - carry : P - carry],
                                scalar=coef(o, h),
                                in1=accp[:, r0 : r0 + cnt, lo:P],
                                op0=ALU.mult, op1=ALU.add,
                            )
                for q in range(4):
                    for i0, cnt, r0, carry in runs(q, LAST_TAP):
                        nc.vector.scalar_tensor_tensor(
                            out=nat_view[:, carry:P, r0 : r0 + cnt],
                            in0=tps[q][:, i0 : i0 + cnt, 0 : P - carry].rearrange("p i a -> p a i"),
                            scalar=coef(LAST_TAP, h),
                            in1=accp[:, r0 : r0 + cnt, carry:P].rearrange("p r a -> p a r"),
                            op0=ALU.mult, op1=ALU.add,
                        )
                        if carry:
                            nc.vector.tensor_copy(
                                out=nat_view[:, 0:carry, r0 : r0 + cnt],
                                in_=accp[:, r0 : r0 + cnt, 0:carry].rearrange("p r a -> p a r"),
                            )
                for k, o in enumerate(head_taps):
                    nc.gpsimd.tensor_tensor(
                        out=nat[:, o:HEAD], in0=nat[:, o:HEAD], in1=s_head[:, k, 0 : HEAD - o], op=ALU.add
                    )
                for o, up in g_taps:
                    nc.gpsimd.tensor_tensor(out=nat[:, o:up], in0=nat[:, o:up], in1=scaled[o][:, 0 : up - o], op=ALU.add)
                for b2 in range(2):
                    nc.sync.dma_start(
                        out=out[2 * pair + b2, h * HD : (h + 1) * HD, :], in_=nat[b2 * HD : (b2 + 1) * HD, :]
                    )

            for u in range(UNITS):
                unit(u)
